import numpy as np
import ml_dtypes


def mxq(x, axis, fmt="e4m3"):
    dtype, down = {"e4m3": (ml_dtypes.float8_e4m3fn, 7), "e5m2": (ml_dtypes.float8_e5m2, 14)}[fmt]
    v = np.moveaxis(np.asarray(x, np.float32).astype(ml_dtypes.bfloat16).astype(np.float64), axis, -1)
    blocks = v.reshape(v.shape[:-1] + (-1, 32))
    amax = np.abs(blocks).max(-1, keepdims=True)
    byte = np.maximum(np.where(amax > 0, np.frexp(amax)[1] - 1 + 127, 0) - down, 1)
    scale = np.exp2(byte - 127.0)
    codes = (blocks / scale).astype(np.float32).astype(dtype).astype(np.float64)
    return np.moveaxis((codes * scale).reshape(v.shape), -1, axis)


WIDE = False


def mx_kscale(k):
    if not WIDE:
        return np.ones(k)
    levels = np.array([10, -10, 5, -5, 0])
    a = np.random.permutation(np.resize(levels, k // 512 * 4)).reshape(k // 512, 4)
    idx = np.arange(k)
    return np.exp2(a[idx // 512, idx % 128 // 32])


BF16 = ml_dtypes.bfloat16


def bf(x):
    return np.asarray(x, np.float32).astype(BF16)


def f64(x):
    return np.asarray(x).astype(np.float64)


B, T, N, D, KD, VD = 4, 2048, 1024, 128, 512, 512
ITERS = 5
REG = 1.0
SIG = 3.5


def lse(x, axis):
    m = x.max(axis=axis, keepdims=True)
    return m + np.log(np.exp(x - m).sum(axis=axis, keepdims=True))


def setup_inputs():
    s = mx_kscale(VD)
    return {"q_proj": bf(np.random.standard_normal((T, D)) * SIG),
            "k_proj": bf(np.random.standard_normal((B, N, D)) * SIG),
            "v": bf(np.random.standard_normal((B, N, VD)) * s),
            "w_v": bf(np.random.standard_normal((VD, D)) * 1.5 / np.sqrt(VD) / s[:, None])}


def reference(q_proj, k_proj, v, w_v):
    q2 = (f64(q_proj) * f64(q_proj)).sum(-1)
    k2 = (f64(k_proj) * f64(k_proj)).sum(-1)
    qk = f64(q_proj) @ f64(k_proj).transpose(0, 2, 1)
    sq = q2[None, :, None] + k2[:, None, :] - 2.0 * qk
    logk = -np.sqrt(np.maximum(sq, 0.0)) / REG
    log_a = -np.log(N)
    log_b = 0.0
    g = np.zeros((B, T, 1))
    for _ in range(ITERS):
        f = log_a - lse(logk + g, 1)
        g = log_b - lse(logk + f, 2)
    pi = np.exp(logk + f + g)
    vp = mxq(f64(v), 2, "e4m3") @ mxq(f64(w_v), 0, "e4m3")
    return mxq(pi, 2, "e4m3") @ mxq(vp, 1, "e4m3")

@@ -1,0 +1,212 @@
+from contextlib import ExitStack
+
+import concourse.mybir as mybir
+from concourse.masks import make_identity
+
+F32 = mybir.dt.float32
+BF16 = mybir.dt.bfloat16
+U32 = mybir.dt.uint32
+U8 = mybir.dt.uint8
+FP8X4 = mybir.dt.float8_e4m3fn_x4
+ACT = mybir.ActivationFunctionType
+ALU = mybir.AluOpType
+AX = mybir.AxisListType
+
+B, T, N, D, VD = 4, 2048, 1024, 128, 512
+ITERS = 5
+P = 128
+NT = N // P
+TT = T // P
+FLOPS = 2 * B * (2 * T * N * D + N * VD * D)
+
+VECTOR_SCALES = (3, 7)
+
+
+def tile_sinkhornattention_pa_t_kernel(tc, q_proj, k_proj, v, w_v, out):
+    nc = tc.nc
+    with ExitStack() as ctx:
+        const = ctx.enter_context(tc.tile_pool(name="const", bufs=1))
+        ps_a = ctx.enter_context(tc.psum_pool(name="ps_a", bufs=1))
+        ps_s = ctx.enter_context(tc.psum_pool(name="ps_s", bufs=2))
+        ps_w = ctx.enter_context(tc.psum_pool(name="ps_w", bufs=2))
+
+        ident_f = const.tile([P, P], F32, name="ident_f")
+        make_identity(nc, ident_f[:])
+        ident_b = const.tile([P, P], BF16, name="ident_b")
+        make_identity(nc, ident_b[:])
+        q_t = const.tile([P, T], BF16, name="q_t")
+        nq2h = const.tile([P, TT], F32, name="nq2h")
+        vp_codes = const.tile([P, B, 2, P], U32, name="vp_codes", align_bytes=64)
+        vp_scales = const.tile([P, B, 2, P], U8, name="vp_scales", align_bytes=64)
+
+        with tc.tile_pool(name="prep", bufs=1) as prep, tc.tile_pool(name="prep2", bufs=2) as prep2:
+            q_sb = prep.tile([P, TT, D], BF16, name="q_sb")
+            nc.sync.dma_start(out=q_sb[:], in_=q_proj.rearrange("(p a) d -> p a d", a=TT))
+            wv_sb = prep.tile([P, 2, 2, D], BF16, name="wv_sb")
+            nc.sync.dma_start(out=wv_sb[:], in_=w_v.rearrange("(u q e) c -> q u e c", u=2, e=2))
+
+            q_sq = prep.tile([P, TT, D], F32, name="q_sq")
+            nc.vector.tensor_tensor(out=q_sq[:], in0=q_sb[:], in1=q_sb[:], op=ALU.mult)
+            q2 = prep.tile([P, TT], F32, name="q2")
+            nc.vector.tensor_reduce(out=q2[:], in_=q_sq[:], axis=AX.X, op=ALU.add)
+            nc.vector.tensor_scalar(out=nq2h[:], in0=q2[:], scalar1=-0.5, scalar2=None, op0=ALU.mult)
+            for g in range(4):
+                pt = ps_s.tile([P, 512], BF16, name="pt", tag="s")
+                for a in range(4):
+                    nc.tensor.transpose(pt[:, a * P:(a + 1) * P], q_sb[:, 4 * g + a, :], ident_b[:])
+                nc.vector.tensor_copy(out=q_t[:, g * 512:(g + 1) * 512], in_=pt[:])
+
+            wv_grp = prep.tile([P, D, 4], BF16, name="wv_grp", align_bytes=64)
+            nc.vector.tensor_copy(out=wv_grp[:], in_=wv_sb[:].rearrange("q u e c -> q c (u e)"))
+            wv_codes = prep.tile([P, D], U32, name="wv_codes", align_bytes=64)
+            wv_scales = prep.tile([P, D], U8, name="wv_scales", align_bytes=64)
+            nc.vector.quantize_mx(
+                out=wv_codes[:].bitcast(FP8X4), scales=wv_scales[:],
+                in_=wv_grp[:].rearrange("q c t -> q (c t)"))
+
+            for b in range(B):
+                v_sb = prep2.tile([P, 2, 4, VD], BF16, name="v_sb")
+                nc.sync.dma_start(out=v_sb[:], in_=v[b].rearrange("(c p j) f -> p c j f", c=2, j=4))
+                for c in range(2):
+                    v_grp = prep2.tile([P, 4 * P * 4], BF16, name="v_grp", align_bytes=64)
+                    v_words = v_grp[:].bitcast(F32).rearrange("q (j n u) -> q j n u", j=4, u=2)
+                    for h in range(2):
+                        pv = ps_s.tile([P, 2, 2, P], F32, name="pv", tag="s")
+                        for jj in range(2):
+                            words = v_sb[:, c, 2 * h + jj, :].bitcast(F32)
+                            for u in range(2):
+                                nc.tensor.transpose(pv[:, jj, u, :], words[:, u * P:(u + 1) * P], ident_f[:])
+                        nc.vector.tensor_copy(
+                            out=v_words[:, 2 * h:2 * h + 2, :, :],
+                            in_=pv[:].rearrange("q j u n -> q j n u"))
+                    v_codes = prep2.tile([P, 4 * P], U32, name="v_codes", align_bytes=64)
+                    v_scales = prep2.tile([P, 4 * P], U8, name="v_scales", align_bytes=64)
+                    nc.vector.quantize_mx(out=v_codes[:].bitcast(FP8X4), scales=v_scales[:], in_=v_grp[:])
+                    pvp = ps_w.tile([P, 4, D], F32, name="pvp", tag="w")
+                    for j in range(4):
+                        nc.tensor.matmul_mx(
+                            out=pvp[:, j, :],
+                            lhsT=v_codes[:, j * P:(j + 1) * P].bitcast(FP8X4),
+                            lhsT_scale=v_scales[:, j * P:(j + 1) * P],
+                            rhs=wv_codes[:].bitcast(FP8X4), rhs_scale=wv_scales[:],
+                            start=True, stop=True)
+                    vp_grp = prep2.tile([P, D, 4], BF16, name="vp_grp", align_bytes=64)
+                    nc.vector.tensor_copy(out=vp_grp[:], in_=pvp[:].rearrange("p j d -> p d j"))
+                    nc.vector.quantize_mx(
+                        out=vp_codes[:, b, c, :].bitcast(FP8X4), scales=vp_scales[:, b, c, :],
+                        in_=vp_grp[:].rearrange("p d j -> p (d j)"))
+
+        kern = ctx.enter_context(tc.tile_pool(name="kern", bufs=4))
+        keys = ctx.enter_context(tc.tile_pool(name="keys", bufs=2))
+        small = ctx.enter_context(tc.tile_pool(name="small", bufs=4))
+        wide = ctx.enter_context(tc.tile_pool(name="wide", bufs=2))
+        one = ctx.enter_context(tc.tile_pool(name="one", bufs=1))
+
+        for b in range(B):
+            k_sb = keys.tile([P, NT, D], BF16, name="k_sb")
+            nc.sync.dma_start(
+                out=k_sb[:].rearrange("p (c j) d -> p c j d", c=2),
+                in_=k_proj[b].rearrange("(c p j) d -> p c j d", c=2, j=4))
+            k_sq = one.tile([P, NT, D], F32, name="k_sq")
+            nc.vector.tensor_tensor(out=k_sq[:], in0=k_sb[:], in1=k_sb[:], op=ALU.mult)
+            k2 = small.tile([P, NT], F32, name="k2")
+            nc.vector.tensor_reduce(out=k2[:], in_=k_sq[:], axis=AX.X, op=ALU.add)
+            k_t = keys.tile([P, NT, P], BF16, name="k_t")
+            for g in range(2):
+                pk = ps_s.tile([P, 4, P], BF16, name="pk", tag="s")
+                for a in range(4):
+                    nc.tensor.transpose(pk[:, a, :], k_sb[:, 4 * g + a, :], ident_b[:])
+                nc.vector.tensor_copy(out=k_t[:, 4 * g:4 * g + 4, :], in_=pk[:])
+
+            halves = [kern.tile([P, 4, T], F32, name="half%d" % c, tag="half") for c in range(2)]
+
+            def rows(i):
+                return halves[i // 4][:, i % 4, :]
+
+            sq_min = small.tile([P, NT], F32, name="sq_min")
+            for i in range(NT):
+                for ch in range(4):
+                    ps = ps_s.tile([P, 512], F32, name="ps", tag="s")
+                    nc.tensor.matmul(ps[:], lhsT=k_t[:, i, :], rhs=q_t[:, ch * 512:(ch + 1) * 512],
+                                     start=True, stop=False)
+                    for a in range(4):
+                        col = 4 * ch + a
+                        nc.tensor.matmul(ps[:, a * P:(a + 1) * P],
+                                         lhsT=nq2h[:, col:col + 1].to_broadcast([P, P]), rhs=ident_f[:],
+                                         is_transpose=True, start=False, stop=(a == 3))
+                    nc.scalar.activation(out=rows(i)[:, ch * 512:(ch + 1) * 512], in_=ps[:], func=ACT.Relu,
+                                         bias=k2[:, i:i + 1], scale=-2.0)
+                nc.vector.tensor_reduce(out=sq_min[:, i:i + 1], in_=rows(i), axis=AX.X, op=ALU.min)
+            shift = small.tile([P, NT], F32, name="shift")
+            nc.scalar.activation(out=shift[:], in_=sq_min[:], func=ACT.Sqrt)
+            for i in range(NT):
+                nc.scalar.activation(out=rows(i), in_=rows(i), func=ACT.Sqrt)
+            s_first = small.tile([P, NT], F32, name="s_first")
+            for i in range(NT):
+                nc.scalar.activation(out=rows(i), in_=rows(i), func=ACT.Exp, bias=shift[:, i:i + 1], scale=-1.0,
+                                     accum_out=s_first[:, i:i + 1])
+            s_n = small.tile([P, NT], F32, name="s_n")
+            nc.vector.tensor_scalar(out=s_n[:], in0=s_first[:], scalar1=float(N), scalar2=None, op0=ALU.mult)
+
+            w_all = None
+            for it in range(ITERS):
+                rho = small.tile([P, NT], F32, name="rho")
+                acc = ps_a.tile([P, TT, P], F32, name="acc")
+                for i in range(NT):
+                    if it > 0:
+                        junk = one.tile([P, T], BF16, name="junk")
+                        nc.vector.scalar_tensor_tensor(
+                            out=junk[:], in0=rows(i), scalar=float(N), in1=w_all[:],
+                            op0=ALU.mult, op1=ALU.mult, accum_out=s_n[:, i:i + 1])
+                    nc.vector.reciprocal(out=rho[:, i:i + 1], in_=s_n[:, i:i + 1])
+                    if i in VECTOR_SCALES:
+                        nc.vector.tensor_scalar(out=rows(i), in0=rows(i), scalar1=rho[:, i:i + 1], scalar2=None,
+                                                op0=ALU.mult)
+                    else:
+                        nc.scalar.activation(out=rows(i), in_=rows(i), func=ACT.Copy, scale=rho[:, i:i + 1])
+                    for a in range(TT):
+                        nc.tensor.matmul(acc[:, a, :], lhsT=rows(i)[:, a * P:(a + 1) * P], rhs=ident_f[:],
+                                         is_transpose=True,
+                                         start=(i == 0 and a % 4 == 0), stop=(i == NT - 1 and a % 4 == 3))
+                r_sum = small.tile([P, TT], F32, name="r_sum")
+                for g in range(4):
+                    nc.vector.tensor_reduce(out=r_sum[:, 4 * g:4 * g + 4], in_=acc[:, 4 * g:4 * g + 4, :],
+                                            axis=AX.X, op=ALU.add)
+                w_col = small.tile([P, TT], F32, name="w_col")
+                nc.vector.reciprocal(out=w_col[:], in_=r_sum[:])
+                w_all = wide.tile([P, T], F32, name="w_all")
+                for g in range(4):
+                    pw = ps_w.tile([P, 512], F32, name="pw", tag="w")
+                    for a in range(4):
+                        col = 4 * g + a
+                        nc.tensor.transpose(pw[:, a * P:(a + 1) * P],
+                                            w_col[:, col:col + 1].to_broadcast([P, P]), ident_f[:])
+                    nc.scalar.copy(out=w_all[:, g * 512:(g + 1) * 512], in_=pw[:])
+                if it < ITERS - 1:
+                    s_n = small.tile([P, NT], F32, name="s_n")
+
+            out_view = out[b].rearrange("(p a) d -> p a d", a=TT)
+            for g in range(4):
+                codes = wide.tile([P, 2, 512], U32, name="codes", align_bytes=64)
+                scales = wide.tile([P, 2, 512], U8, name="scales", align_bytes=64)
+                for c in range(2):
+                    grp = wide.tile([P, 512, 4], BF16, name="grp", align_bytes=64)
+                    nc.vector.tensor_tensor(
+                        out=grp[:],
+                        in0=halves[c][:, :, g * 512:(g + 1) * 512].rearrange("p j t -> p t j"),
+                        in1=w_all[:, g * 512:(g + 1) * 512].unsqueeze(2).to_broadcast([P, 512, 4]),
+                        op=ALU.mult)
+                    nc.vector.quantize_mx(out=codes[:, c, :].bitcast(FP8X4), scales=scales[:, c, :],
+                                          in_=grp[:].rearrange("p t j -> p (t j)"))
+                po = ps_w.tile([P, 4, D], F32, name="po", tag="w")
+                for a in range(4):
+                    for c in range(2):
+                        nc.tensor.matmul_mx(
+                            out=po[:, a, :],
+                            lhsT=codes[:, c, a * P:(a + 1) * P].bitcast(FP8X4),
+                            lhsT_scale=scales[:, c, a * P:(a + 1) * P],
+                            rhs=vp_codes[:, b, c, :].bitcast(FP8X4), rhs_scale=vp_scales[:, b, c, :],
+                            start=(c == 0), stop=(c == 1))
+                o_sb = wide.tile([P, 4, D], F32, name="o_sb")
+                nc.scalar.copy(out=o_sb[:], in_=po[:])
+                nc.sync.dma_start(out=out_view[:, 4 * g:4 * g + 4, :], in_=o_sb[:])

@@ -18,195 +18,260 @@ P = 128
 NT = N // P
 TT = T // P
 FLOPS = 2 * B * (2 * T * N * D + N * VD * D)
-
-VECTOR_SCALES = (3, 7)
+LAG = 0
 
 
 def tile_sinkhornattention_pa_t_kernel(tc, q_proj, k_proj, v, w_v, out):
     nc = tc.nc
     with ExitStack() as ctx:
         const = ctx.enter_context(tc.tile_pool(name="const", bufs=1))
+        kern = ctx.enter_context(tc.tile_pool(name="kern", bufs=4))
+        keys = ctx.enter_context(tc.tile_pool(name="keys", bufs=2))
+        small = ctx.enter_context(tc.tile_pool(name="small", bufs=4))
+        wide = ctx.enter_context(tc.tile_pool(name="wide", bufs=2))
+        one = ctx.enter_context(tc.tile_pool(name="one", bufs=1))
         ps_a = ctx.enter_context(tc.psum_pool(name="ps_a", bufs=1))
-        ps_s = ctx.enter_context(tc.psum_pool(name="ps_s", bufs=2))
-        ps_w = ctx.enter_context(tc.psum_pool(name="ps_w", bufs=2))
+        ps = ctx.enter_context(tc.psum_pool(name="ps", bufs=4))
 
         ident_f = const.tile([P, P], F32, name="ident_f")
         make_identity(nc, ident_f[:])
         ident_b = const.tile([P, P], BF16, name="ident_b")
         make_identity(nc, ident_b[:])
         q_t = const.tile([P, T], BF16, name="q_t")
-        nq2h = const.tile([P, TT], F32, name="nq2h")
+        q2_all = const.tile([P, T], F32, name="q2_all")
         vp_codes = const.tile([P, B, 2, P], U32, name="vp_codes", align_bytes=64)
         vp_scales = const.tile([P, B, 2, P], U8, name="vp_scales", align_bytes=64)
+        wv_codes = const.tile([P, D], U32, name="wv_codes", align_bytes=64)
+        wv_scales = const.tile([P, D], U8, name="wv_scales", align_bytes=64)
 
-        with tc.tile_pool(name="prep", bufs=1) as prep, tc.tile_pool(name="prep2", bufs=2) as prep2:
-            q_sb = prep.tile([P, TT, D], BF16, name="q_sb")
-            nc.sync.dma_start(out=q_sb[:], in_=q_proj.rearrange("(p a) d -> p a d", a=TT))
-            wv_sb = prep.tile([P, 2, 2, D], BF16, name="wv_sb")
-            nc.sync.dma_start(out=wv_sb[:], in_=w_v.rearrange("(u q e) c -> q u e c", u=2, e=2))
+        state = [dict() for b in range(B)]
+        waiting = []
 
-            q_sq = prep.tile([P, TT, D], F32, name="q_sq")
-            nc.vector.tensor_tensor(out=q_sq[:], in0=q_sb[:], in1=q_sb[:], op=ALU.mult)
-            q2 = prep.tile([P, TT], F32, name="q2")
-            nc.vector.tensor_reduce(out=q2[:], in_=q_sq[:], axis=AX.X, op=ALU.add)
-            nc.vector.tensor_scalar(out=nq2h[:], in0=q2[:], scalar1=-0.5, scalar2=None, op0=ALU.mult)
+        def step(first, later=None):
+            first()
+            waiting.append(later)
+            if len(waiting) > LAG:
+                due = waiting.pop(0)
+                if due is not None:
+                    due()
+
+        def rows(b, i):
+            return state[b]["half"][i // 4][:, i % 4, :]
+
+        def spread(col, dest):
             for g in range(4):
-                pt = ps_s.tile([P, 512], BF16, name="pt", tag="s")
+                pw = ps.tile([P, 512], F32, name="pw", tag="ps")
                 for a in range(4):
-                    nc.tensor.transpose(pt[:, a * P:(a + 1) * P], q_sb[:, 4 * g + a, :], ident_b[:])
-                nc.vector.tensor_copy(out=q_t[:, g * 512:(g + 1) * 512], in_=pt[:])
+                    nc.tensor.transpose(pw[:, a * P:(a + 1) * P],
+                                        col[:, 4 * g + a:4 * g + a + 1].to_broadcast([P, P]), ident_f[:])
+                nc.scalar.copy(out=dest[:, g * 512:(g + 1) * 512], in_=pw[:])
 
-            wv_grp = prep.tile([P, D, 4], BF16, name="wv_grp", align_bytes=64)
+        q_sb = one.tile([P, TT, D], BF16, name="q_sb", tag="j4")
+        nc.sync.dma_start(out=q_sb[:], in_=q_proj.rearrange("(p a) d -> p a d", a=TT))
+        k_all = const.tile([P, B, NT, D], BF16, name="k_all")
+        for b in range(B):
+            nc.sync.dma_start(
+                out=k_all[:, b, :, :].rearrange("p (c j) d -> p c j d", c=2),
+                in_=k_proj[b].rearrange("(c p j) d -> p c j d", c=2, j=4))
+        for g in range(4):
+            pt = ps.tile([P, 512], BF16, name="pt", tag="ps")
+            for a in range(4):
+                nc.tensor.transpose(pt[:, a * P:(a + 1) * P], q_sb[:, 4 * g + a, :], ident_b[:])
+            nc.vector.tensor_copy(out=q_t[:, g * 512:(g + 1) * 512], in_=pt[:])
+        q_sq = wide.tile([P, TT, D], F32, name="q_sq", tag="w8")
+        nc.vector.tensor_tensor(out=q_sq[:], in0=q_sb[:], in1=q_sb[:], op=ALU.mult)
+        q2 = small.tile([P, TT], F32, name="q2")
+        nc.vector.tensor_reduce(out=q2[:], in_=q_sq[:], axis=AX.X, op=ALU.add)
+        spread(q2, q2_all)
+
+        def wv_step():
+            wv_sb = one.tile([P, 2, 2, D], BF16, name="wv_sb")
+            nc.sync.dma_start(out=wv_sb[:], in_=w_v.rearrange("(u q e) c -> q u e c", u=2, e=2))
+            wv_grp = one.tile([P, D, 4], BF16, name="wv_grp", align_bytes=64)
             nc.vector.tensor_copy(out=wv_grp[:], in_=wv_sb[:].rearrange("q u e c -> q c (u e)"))
-            wv_codes = prep.tile([P, D], U32, name="wv_codes", align_bytes=64)
-            wv_scales = prep.tile([P, D], U8, name="wv_scales", align_bytes=64)
             nc.vector.quantize_mx(
                 out=wv_codes[:].bitcast(FP8X4), scales=wv_scales[:],
                 in_=wv_grp[:].rearrange("q c t -> q (c t)"))
 
+        def vp_step(b, c):
+            if c == 0:
+                v_new = wide.tile([P, 2, 4, VD], BF16, name="v_sb", tag="w8")
+                nc.sync.dma_start(out=v_new[:], in_=v[b].rearrange("(c p j) f -> p c j f", c=2, j=4))
+                state[b]["v_sb"] = v_new
+            v_sb = state[b]["v_sb"]
+            v_grp = wide.tile([P, 4 * P * 4], BF16, name="v_grp", tag="g4", align_bytes=64)
+            v_words = v_grp[:].bitcast(F32).rearrange("q (j n u) -> q j n u", j=4, u=2)
+            for h in range(2):
+                pv = ps.tile([P, 2, 2, P], F32, name="pv", tag="ps")
+                for jj in range(2):
+                    words = v_sb[:, c, 2 * h + jj, :].bitcast(F32)
+                    for u in range(2):
+                        nc.tensor.transpose(pv[:, jj, u, :], words[:, u * P:(u + 1) * P], ident_f[:])
+                nc.vector.tensor_copy(
+                    out=v_words[:, 2 * h:2 * h + 2, :, :],
+                    in_=pv[:].rearrange("q j u n -> q j n u"))
+            v_codes = wide.tile([P, 4 * P], U32, name="v_codes", tag="codes", align_bytes=64)
+            v_scales = wide.tile([P, 4 * P], U8, name="v_scales", tag="scales", align_bytes=64)
+            nc.vector.quantize_mx(out=v_codes[:].bitcast(FP8X4), scales=v_scales[:], in_=v_grp[:])
+            pvp = ps.tile([P, 4, D], F32, name="pvp", tag="ps")
+            for j in range(4):
+                nc.tensor.matmul_mx(
+                    out=pvp[:, j, :],
+                    lhsT=v_codes[:, j * P:(j + 1) * P].bitcast(FP8X4),
+                    lhsT_scale=v_scales[:, j * P:(j + 1) * P],
+                    rhs=wv_codes[:].bitcast(FP8X4), rhs_scale=wv_scales[:],
+                    start=True, stop=True)
+            vp_grp = one.tile([P, D, 4], BF16, name="vp_grp", align_bytes=64)
+            nc.vector.tensor_copy(out=vp_grp[:], in_=pvp[:].rearrange("p j d -> p d j"))
+            nc.vector.quantize_mx(
+                out=vp_codes[:, b, c, :].bitcast(FP8X4), scales=vp_scales[:, b, c, :],
+                in_=vp_grp[:].rearrange("p d j -> p (d j)"))
+
+        def value_projection():
+            step(wv_step)
             for b in range(B):
-                v_sb = prep2.tile([P, 2, 4, VD], BF16, name="v_sb")
-                nc.sync.dma_start(out=v_sb[:], in_=v[b].rearrange("(c p j) f -> p c j f", c=2, j=4))
                 for c in range(2):
-                    v_grp = prep2.tile([P, 4 * P * 4], BF16, name="v_grp", align_bytes=64)
-                    v_words = v_grp[:].bitcast(F32).rearrange("q (j n u) -> q j n u", j=4, u=2)
-                    for h in range(2):
-                        pv = ps_s.tile([P, 2, 2, P], F32, name="pv", tag="s")
-                        for jj in range(2):
-                            words = v_sb[:, c, 2 * h + jj, :].bitcast(F32)
-                            for u in range(2):
-                                nc.tensor.transpose(pv[:, jj, u, :], words[:, u * P:(u + 1) * P], ident_f[:])
-                        nc.vector.tensor_copy(
-                            out=v_words[:, 2 * h:2 * h + 2, :, :],
-                            in_=pv[:].rearrange("q j u n -> q j n u"))
-                    v_codes = prep2.tile([P, 4 * P], U32, name="v_codes", align_bytes=64)
-                    v_scales = prep2.tile([P, 4 * P], U8, name="v_scales", align_bytes=64)
-                    nc.vector.quantize_mx(out=v_codes[:].bitcast(FP8X4), scales=v_scales[:], in_=v_grp[:])
-                    pvp = ps_w.tile([P, 4, D], F32, name="pvp", tag="w")
-                    for j in range(4):
-                        nc.tensor.matmul_mx(
-                            out=pvp[:, j, :],
-                            lhsT=v_codes[:, j * P:(j + 1) * P].bitcast(FP8X4),
-                            lhsT_scale=v_scales[:, j * P:(j + 1) * P],
-                            rhs=wv_codes[:].bitcast(FP8X4), rhs_scale=wv_scales[:],
-                            start=True, stop=True)
-                    vp_grp = prep2.tile([P, D, 4], BF16, name="vp_grp", align_bytes=64)
-                    nc.vector.tensor_copy(out=vp_grp[:], in_=pvp[:].rearrange("p j d -> p d j"))
-                    nc.vector.quantize_mx(
-                        out=vp_codes[:, b, c, :].bitcast(FP8X4), scales=vp_scales[:, b, c, :],
-                        in_=vp_grp[:].rearrange("p d j -> p (d j)"))
+                    step(lambda b=b, c=c: vp_step(b, c))
 
-        kern = ctx.enter_context(tc.tile_pool(name="kern", bufs=4))
-        keys = ctx.enter_context(tc.tile_pool(name="keys", bufs=2))
-        small = ctx.enter_context(tc.tile_pool(name="small", bufs=4))
-        wide = ctx.enter_context(tc.tile_pool(name="wide", bufs=2))
-        one = ctx.enter_context(tc.tile_pool(name="one", bufs=1))
-
-        for b in range(B):
-            k_sb = keys.tile([P, NT, D], BF16, name="k_sb")
-            nc.sync.dma_start(
-                out=k_sb[:].rearrange("p (c j) d -> p c j d", c=2),
-                in_=k_proj[b].rearrange("(c p j) d -> p c j d", c=2, j=4))
+        def keys_step(b):
+            st = state[b]
+            k_sb = k_all[:, b, :, :]
             k_sq = one.tile([P, NT, D], F32, name="k_sq")
-            nc.vector.tensor_tensor(out=k_sq[:], in0=k_sb[:], in1=k_sb[:], op=ALU.mult)
+            nc.vector.tensor_tensor(out=k_sq[:], in0=k_sb, in1=k_sb, op=ALU.mult)
             k2 = small.tile([P, NT], F32, name="k2")
             nc.vector.tensor_reduce(out=k2[:], in_=k_sq[:], axis=AX.X, op=ALU.add)
+            nk2 = small.tile([P, NT], F32, name="nk2")
+            nc.vector.tensor_scalar(out=nk2[:], in0=k2[:], scalar1=-1.0, scalar2=None, op0=ALU.mult)
             k_t = keys.tile([P, NT, P], BF16, name="k_t")
             for g in range(2):
-                pk = ps_s.tile([P, 4, P], BF16, name="pk", tag="s")
+                pk = ps.tile([P, 4, P], BF16, name="pk", tag="ps")
                 for a in range(4):
                     nc.tensor.transpose(pk[:, a, :], k_sb[:, 4 * g + a, :], ident_b[:])
                 nc.vector.tensor_copy(out=k_t[:, 4 * g:4 * g + 4, :], in_=pk[:])
+            st["k2"] = k2
+            st["nk2"] = nk2
+            st["k_t"] = k_t
+            st["half"] = []
+            st["x_min"] = small.tile([P, NT], F32, name="x_min")
+            st["s_first"] = small.tile([P, NT], F32, name="s_first")
 
-            halves = [kern.tile([P, 4, T], F32, name="half%d" % c, tag="half") for c in range(2)]
+        def dist_step(b, i):
+            st = state[b]
+            if i % 4 == 0:
+                st["half"].append(kern.tile([P, 4, T], F32, name="half", tag="half"))
+            for ch in range(4):
+                pd = ps.tile([P, 512], F32, name="pd", tag="ps")
+                nc.tensor.matmul(pd[:], lhsT=st["k_t"][:, i, :], rhs=q_t[:, ch * 512:(ch + 1) * 512],
+                                 start=True, stop=True)
+                nc.vector.scalar_tensor_tensor(
+                    out=rows(b, i)[:, ch * 512:(ch + 1) * 512], in0=pd[:], scalar=-2.0,
+                    in1=q2_all[:, ch * 512:(ch + 1) * 512], op0=ALU.mult, op1=ALU.add)
+            nc.vector.tensor_scalar(out=rows(b, i), in0=rows(b, i), scalar1=st["nk2"][:, i:i + 1], scalar2=None,
+                                    op0=ALU.max, op1=ALU.min, accum_out=st["x_min"][:, i:i + 1])
+            nc.scalar.activation(out=rows(b, i), in_=rows(b, i), func=ACT.Sqrt, bias=st["k2"][:, i:i + 1])
 
-            def rows(i):
-                return halves[i // 4][:, i % 4, :]
-
+        def shift_step(b):
+            st = state[b]
             sq_min = small.tile([P, NT], F32, name="sq_min")
-            for i in range(NT):
-                for ch in range(4):
-                    ps = ps_s.tile([P, 512], F32, name="ps", tag="s")
-                    nc.tensor.matmul(ps[:], lhsT=k_t[:, i, :], rhs=q_t[:, ch * 512:(ch + 1) * 512],
-                                     start=True, stop=False)
-                    for a in range(4):
-                        col = 4 * ch + a
-                        nc.tensor.matmul(ps[:, a * P:(a + 1) * P],
-                                         lhsT=nq2h[:, col:col + 1].to_broadcast([P, P]), rhs=ident_f[:],
-                                         is_transpose=True, start=False, stop=(a == 3))
-                    nc.scalar.activation(out=rows(i)[:, ch * 512:(ch + 1) * 512], in_=ps[:], func=ACT.Relu,
-                                         bias=k2[:, i:i + 1], scale=-2.0)
-                nc.vector.tensor_reduce(out=sq_min[:, i:i + 1], in_=rows(i), axis=AX.X, op=ALU.min)
-            shift = small.tile([P, NT], F32, name="shift")
-            nc.scalar.activation(out=shift[:], in_=sq_min[:], func=ACT.Sqrt)
-            for i in range(NT):
-                nc.scalar.activation(out=rows(i), in_=rows(i), func=ACT.Sqrt)
-            s_first = small.tile([P, NT], F32, name="s_first")
-            for i in range(NT):
-                nc.scalar.activation(out=rows(i), in_=rows(i), func=ACT.Exp, bias=shift[:, i:i + 1], scale=-1.0,
-                                     accum_out=s_first[:, i:i + 1])
-            s_n = small.tile([P, NT], F32, name="s_n")
-            nc.vector.tensor_scalar(out=s_n[:], in0=s_first[:], scalar1=float(N), scalar2=None, op0=ALU.mult)
+            nc.vector.tensor_tensor(out=sq_min[:], in0=st["x_min"][:], in1=st["k2"][:], op=ALU.add)
+            st["shift"] = small.tile([P, NT], F32, name="shift")
+            nc.scalar.activation(out=st["shift"][:], in_=sq_min[:], func=ACT.Sqrt)
 
-            w_all = None
-            for it in range(ITERS):
-                rho = small.tile([P, NT], F32, name="rho")
-                acc = ps_a.tile([P, TT, P], F32, name="acc")
-                for i in range(NT):
-                    if it > 0:
-                        junk = one.tile([P, T], BF16, name="junk")
-                        nc.vector.scalar_tensor_tensor(
-                            out=junk[:], in0=rows(i), scalar=float(N), in1=w_all[:],
-                            op0=ALU.mult, op1=ALU.mult, accum_out=s_n[:, i:i + 1])
-                    nc.vector.reciprocal(out=rho[:, i:i + 1], in_=s_n[:, i:i + 1])
-                    if i in VECTOR_SCALES:
-                        nc.vector.tensor_scalar(out=rows(i), in0=rows(i), scalar1=rho[:, i:i + 1], scalar2=None,
-                                                op0=ALU.mult)
-                    else:
-                        nc.scalar.activation(out=rows(i), in_=rows(i), func=ACT.Copy, scale=rho[:, i:i + 1])
-                    for a in range(TT):
-                        nc.tensor.matmul(acc[:, a, :], lhsT=rows(i)[:, a * P:(a + 1) * P], rhs=ident_f[:],
-                                         is_transpose=True,
-                                         start=(i == 0 and a % 4 == 0), stop=(i == NT - 1 and a % 4 == 3))
+        def distances(b):
+            step(lambda: keys_step(b))
+            for i in range(NT):
+                step(lambda i=i: dist_step(b, i))
+            step(lambda: shift_step(b))
+
+        def tile_front(b, it, i):
+            st = state[b]
+            if it == 0:
+                nc.scalar.activation(out=rows(b, i), in_=rows(b, i), func=ACT.Exp, bias=st["shift"][:, i:i + 1],
+                                     scale=-1.0, accum_out=st["s_first"][:, i:i + 1])
+                nc.vector.reciprocal(out=st["rho"][:, i:i + 1], in_=st["s_first"][:, i:i + 1])
+                nc.vector.tensor_scalar(out=rows(b, i), in0=rows(b, i), scalar1=st["rho"][:, i:i + 1],
+                                        scalar2=1.0 / N, op0=ALU.mult, op1=ALU.mult)
+            else:
+                junk = one.tile([P, T], BF16, name="junk", tag="j4")
+                nc.vector.scalar_tensor_tensor(
+                    out=junk[:], in0=rows(b, i), scalar=float(N), in1=st["w_all"][:],
+                    op0=ALU.mult, op1=ALU.mult, accum_out=st["s_n"][:, i:i + 1])
+                nc.vector.reciprocal(out=st["rho"][:, i:i + 1], in_=st["s_n"][:, i:i + 1])
+                nc.scalar.activation(out=rows(b, i), in_=rows(b, i), func=ACT.Copy,
+                                     scale=st["rho"][:, i:i + 1])
+
+        def tile_back(b, i):
+            st = state[b]
+            if i == 0:
+                st["acc"] = ps_a.tile([P, TT, P], F32, name="acc")
+            for a in range(TT):
+                nc.tensor.matmul(st["acc"][:, a, :], lhsT=rows(b, i)[:, a * P:(a + 1) * P], rhs=ident_f[:],
+                                 is_transpose=True,
+                                 start=(i == 0 and a % 4 == 0), stop=(i == NT - 1 and a % 4 == 3))
+            if i == NT - 1:
                 r_sum = small.tile([P, TT], F32, name="r_sum")
-                for g in range(4):
-                    nc.vector.tensor_reduce(out=r_sum[:, 4 * g:4 * g + 4], in_=acc[:, 4 * g:4 * g + 4, :],
-                                            axis=AX.X, op=ALU.add)
                 w_col = small.tile([P, TT], F32, name="w_col")
-                nc.vector.reciprocal(out=w_col[:], in_=r_sum[:])
-                w_all = wide.tile([P, T], F32, name="w_all")
+                w_all = wide.tile([P, T], F32, name="w_all", tag="w8")
                 for g in range(4):
-                    pw = ps_w.tile([P, 512], F32, name="pw", tag="w")
-                    for a in range(4):
-                        col = 4 * g + a
-                        nc.tensor.transpose(pw[:, a * P:(a + 1) * P],
-                                            w_col[:, col:col + 1].to_broadcast([P, P]), ident_f[:])
-                    nc.scalar.copy(out=w_all[:, g * 512:(g + 1) * 512], in_=pw[:])
-                if it < ITERS - 1:
-                    s_n = small.tile([P, NT], F32, name="s_n")
+                    nc.vector.tensor_reduce(out=r_sum[:, 4 * g:4 * g + 4], in_=st["acc"][:, 4 * g:4 * g + 4, :],
+                                            axis=AX.X, op=ALU.add)
+                    nc.vector.reciprocal(out=w_col[:, 4 * g:4 * g + 4], in_=r_sum[:, 4 * g:4 * g + 4])
+                spread(w_col, w_all)
+                st["w_all"] = w_all
 
-            out_view = out[b].rearrange("(p a) d -> p a d", a=TT)
-            for g in range(4):
-                codes = wide.tile([P, 2, 512], U32, name="codes", align_bytes=64)
-                scales = wide.tile([P, 2, 512], U8, name="scales", align_bytes=64)
+        def sinkhorn_round(b, it):
+            state[b]["rho"] = small.tile([P, NT], F32, name="rho")
+            state[b]["s_n"] = small.tile([P, NT], F32, name="s_n")
+            for i in range(NT):
+                step(lambda i=i: tile_front(b, it, i), lambda i=i: tile_back(b, i))
+
+        def plan_front(b, g, c):
+            st = state[b]
+            if c == 0:
+                st["codes", g] = wide.tile([P, 2, 512], U32, name="codes", tag="codes", align_bytes=64)
+                st["scales", g] = wide.tile([P, 2, 512], U8, name="scales", tag="scales", align_bytes=64)
+            grp = wide.tile([P, 512, 4], BF16, name="grp", tag="g4", align_bytes=64)
+            nc.vector.tensor_tensor(
+                out=grp[:],
+                in0=st["half"][c][:, :, g * 512:(g + 1) * 512].rearrange("p j t -> p t j"),
+                in1=st["w_all"][:, g * 512:(g + 1) * 512].unsqueeze(2).to_broadcast([P, 512, 4]),
+                op=ALU.mult)
+            nc.vector.quantize_mx(out=st["codes", g][:, c, :].bitcast(FP8X4), scales=st["scales", g][:, c, :],
+                                  in_=grp[:].rearrange("p t j -> p (t j)"))
+
+        def plan_back(b, g):
+            codes = state[b]["codes", g]
+            scales = state[b]["scales", g]
+            po = ps.tile([P, 4, D], F32, name="po", tag="ps")
+            for a in range(4):
                 for c in range(2):
-                    grp = wide.tile([P, 512, 4], BF16, name="grp", align_bytes=64)
-                    nc.vector.tensor_tensor(
-                        out=grp[:],
-                        in0=halves[c][:, :, g * 512:(g + 1) * 512].rearrange("p j t -> p t j"),
-                        in1=w_all[:, g * 512:(g + 1) * 512].unsqueeze(2).to_broadcast([P, 512, 4]),
-                        op=ALU.mult)
-                    nc.vector.quantize_mx(out=codes[:, c, :].bitcast(FP8X4), scales=scales[:, c, :],
-                                          in_=grp[:].rearrange("p t j -> p (t j)"))
-                po = ps_w.tile([P, 4, D], F32, name="po", tag="w")
-                for a in range(4):
-                    for c in range(2):
-                        nc.tensor.matmul_mx(
-                            out=po[:, a, :],
-                            lhsT=codes[:, c, a * P:(a + 1) * P].bitcast(FP8X4),
-                            lhsT_scale=scales[:, c, a * P:(a + 1) * P],
-                            rhs=vp_codes[:, b, c, :].bitcast(FP8X4), rhs_scale=vp_scales[:, b, c, :],
-                            start=(c == 0), stop=(c == 1))
-                o_sb = wide.tile([P, 4, D], F32, name="o_sb")
-                nc.scalar.copy(out=o_sb[:], in_=po[:])
-                nc.sync.dma_start(out=out_view[:, 4 * g:4 * g + 4, :], in_=o_sb[:])
+                    nc.tensor.matmul_mx(
+                        out=po[:, a, :],
+                        lhsT=codes[:, c, a * P:(a + 1) * P].bitcast(FP8X4),
+                        lhsT_scale=scales[:, c, a * P:(a + 1) * P],
+                        rhs=vp_codes[:, b, c, :].bitcast(FP8X4), rhs_scale=vp_scales[:, b, c, :],
+                        start=(c == 0), stop=(c == 1))
+            o_sb = wide.tile([P, 4, D], F32, name="o_sb")
+            nc.scalar.copy(out=o_sb[:], in_=po[:])
+            nc.sync.dma_start(out=out[b].rearrange("(p a) d -> p a d", a=TT)[:, 4 * g:4 * g + 4, :], in_=o_sb[:])
+
+        def attend(b):
+            for g in range(4):
+                step(lambda g=g: plan_front(b, g, 0))
+                step(lambda g=g: plan_front(b, g, 1), lambda g=g: plan_back(b, g))
+
+        for first in range(0, B, 2):
+            pair = (first, first + 1)
+            for b in pair:
+                if first > 0:
+                    attend(b - 2)
+                distances(b)
+            if first == 0:
+                value_projection()
+            for it in range(ITERS):
+                for b in pair:
+                    sinkhorn_round(b, it)
+        for b in (B - 2, B - 1):
+            attend(b)
+        for n in range(LAG):
+            step(lambda: None)

@@ -18,12 +18,13 @@ P = 128
 NT = N // P
 TT = T // P
 FLOPS = 2 * B * (2 * T * N * D + N * VD * D)
-LAG = 0
+LAG = 3
 
 
 def tile_sinkhornattention_pa_t_kernel(tc, q_proj, k_proj, v, w_v, out):
     nc = tc.nc
     with ExitStack() as ctx:
+        ctx.enter_context(tc.manual_schedule())
         const = ctx.enter_context(tc.tile_pool(name="const", bufs=1))
         kern = ctx.enter_context(tc.tile_pool(name="kern", bufs=4))
         keys = ctx.enter_context(tc.tile_pool(name="keys", bufs=2))

@@ -18,7 +18,6 @@ P = 128
 NT = N // P
 TT = T // P
 FLOPS = 2 * B * (2 * T * N * D + N * VD * D)
-LAG = 3
 
 
 def tile_sinkhornattention_pa_t_kernel(tc, q_proj, k_proj, v, w_v, out):
@@ -39,33 +38,26 @@ def tile_sinkhornattention_pa_t_kernel(tc, q_proj, k_proj, v, w_v, out):
         ident_b = const.tile([P, P], BF16, name="ident_b")
         make_identity(nc, ident_b[:])
         q_t = const.tile([P, T], BF16, name="q_t")
-        q2_all = const.tile([P, T], F32, name="q2_all")
+        nq2h = const.tile([P, TT], F32, name="nq2h")
         vp_codes = const.tile([P, B, 2, P], U32, name="vp_codes", align_bytes=64)
         vp_scales = const.tile([P, B, 2, P], U8, name="vp_scales", align_bytes=64)
         wv_codes = const.tile([P, D], U32, name="wv_codes", align_bytes=64)
         wv_scales = const.tile([P, D], U8, name="wv_scales", align_bytes=64)
 
         state = [dict() for b in range(B)]
-        waiting = []
+        pending = []
 
-        def step(first, later=None):
-            first()
-            waiting.append(later)
-            if len(waiting) > LAG:
-                due = waiting.pop(0)
-                if due is not None:
-                    due()
+        def step(*parts):
+            for delay, part in enumerate(parts):
+                while len(pending) <= delay:
+                    pending.append([])
+                if part is not None:
+                    pending[delay].append(part)
+            for part in reversed(pending.pop(0)):
+                part()
 
         def rows(b, i):
             return state[b]["half"][i // 4][:, i % 4, :]
-
-        def spread(col, dest):
-            for g in range(4):
-                pw = ps.tile([P, 512], F32, name="pw", tag="ps")
-                for a in range(4):
-                    nc.tensor.transpose(pw[:, a * P:(a + 1) * P],
-                                        col[:, 4 * g + a:4 * g + a + 1].to_broadcast([P, P]), ident_f[:])
-                nc.scalar.copy(out=dest[:, g * 512:(g + 1) * 512], in_=pw[:])
 
         q_sb = one.tile([P, TT, D], BF16, name="q_sb", tag="j4")
         nc.sync.dma_start(out=q_sb[:], in_=q_proj.rearrange("(p a) d -> p a d", a=TT))
@@ -83,7 +75,7 @@ def tile_sinkhornattention_pa_t_kernel(tc, q_proj, k_proj, v, w_v, out):
         nc.vector.tensor_tensor(out=q_sq[:], in0=q_sb[:], in1=q_sb[:], op=ALU.mult)
         q2 = small.tile([P, TT], F32, name="q2")
         nc.vector.tensor_reduce(out=q2[:], in_=q_sq[:], axis=AX.X, op=ALU.add)
-        spread(q2, q2_all)
+        nc.vector.tensor_scalar(out=nq2h[:], in0=q2[:], scalar1=-0.5, scalar2=None, op0=ALU.mult)
 
         def wv_step():
             wv_sb = one.tile([P, 2, 2, D], BF16, name="wv_sb")
@@ -128,9 +120,10 @@ def tile_sinkhornattention_pa_t_kernel(tc, q_proj, k_proj, v, w_v, out):
                 out=vp_codes[:, b, c, :].bitcast(FP8X4), scales=vp_scales[:, b, c, :],
                 in_=vp_grp[:].rearrange("p d j -> p (d j)"))
 
-        def value_projection():
-            step(wv_step)
-            for b in range(B):
+        def value_projection(pair):
+            if pair[0] == 0:
+                step(wv_step)
+            for b in pair:
                 for c in range(2):
                     step(lambda b=b, c=c: vp_step(b, c))
 
@@ -141,67 +134,83 @@ def tile_sinkhornattention_pa_t_kernel(tc, q_proj, k_proj, v, w_v, out):
             nc.vector.tensor_tensor(out=k_sq[:], in0=k_sb, in1=k_sb, op=ALU.mult)
             k2 = small.tile([P, NT], F32, name="k2")
             nc.vector.tensor_reduce(out=k2[:], in_=k_sq[:], axis=AX.X, op=ALU.add)
-            nk2 = small.tile([P, NT], F32, name="nk2")
-            nc.vector.tensor_scalar(out=nk2[:], in0=k2[:], scalar1=-1.0, scalar2=None, op0=ALU.mult)
             k_t = keys.tile([P, NT, P], BF16, name="k_t")
             for g in range(2):
                 pk = ps.tile([P, 4, P], BF16, name="pk", tag="ps")
                 for a in range(4):
                     nc.tensor.transpose(pk[:, a, :], k_sb[:, 4 * g + a, :], ident_b[:])
                 nc.vector.tensor_copy(out=k_t[:, 4 * g:4 * g + 4, :], in_=pk[:])
+            k2h = small.tile([P, NT], F32, name="k2h")
+            nc.vector.tensor_scalar(out=k2h[:], in0=k2[:], scalar1=0.5, scalar2=None, op0=ALU.mult)
             st["k2"] = k2
-            st["nk2"] = nk2
+            st["k2h"] = k2h
             st["k_t"] = k_t
             st["half"] = []
-            st["x_min"] = small.tile([P, NT], F32, name="x_min")
+            st["y_max"] = small.tile([P, NT, 4], F32, name="y_max")
             st["s_first"] = small.tile([P, NT], F32, name="s_first")
 
-        def dist_step(b, i):
+        def dots(b, i):
             st = state[b]
             if i % 4 == 0:
                 st["half"].append(kern.tile([P, 4, T], F32, name="half", tag="half"))
             for ch in range(4):
                 pd = ps.tile([P, 512], F32, name="pd", tag="ps")
                 nc.tensor.matmul(pd[:], lhsT=st["k_t"][:, i, :], rhs=q_t[:, ch * 512:(ch + 1) * 512],
-                                 start=True, stop=True)
-                nc.vector.scalar_tensor_tensor(
-                    out=rows(b, i)[:, ch * 512:(ch + 1) * 512], in0=pd[:], scalar=-2.0,
-                    in1=q2_all[:, ch * 512:(ch + 1) * 512], op0=ALU.mult, op1=ALU.add)
-            nc.vector.tensor_scalar(out=rows(b, i), in0=rows(b, i), scalar1=st["nk2"][:, i:i + 1], scalar2=None,
-                                    op0=ALU.max, op1=ALU.min, accum_out=st["x_min"][:, i:i + 1])
-            nc.scalar.activation(out=rows(b, i), in_=rows(b, i), func=ACT.Sqrt, bias=st["k2"][:, i:i + 1])
+                                 start=True, stop=False)
+                for a in range(4):
+                    col = 4 * ch + a
+                    nc.tensor.matmul(pd[:, a * P:(a + 1) * P],
+                                     lhsT=nq2h[:, col:col + 1].to_broadcast([P, P]), rhs=ident_f[:],
+                                     is_transpose=True, start=False, stop=(a == 3))
+                nc.vector.tensor_scalar(out=rows(b, i)[:, ch * 512:(ch + 1) * 512], in0=pd[:],
+                                        scalar1=st["k2h"][:, i:i + 1], scalar2=None,
+                                        op0=ALU.min, op1=ALU.max, accum_out=st["y_max"][:, i, ch:ch + 1])
+
+        def root(b, i):
+            nc.scalar.activation(out=rows(b, i), in_=rows(b, i), func=ACT.Sqrt, bias=state[b]["k2"][:, i:i + 1],
+                                 scale=-2.0)
 
         def shift_step(b):
             st = state[b]
+            y_top = small.tile([P, NT], F32, name="y_top")
+            nc.vector.tensor_reduce(out=y_top[:], in_=st["y_max"][:], axis=AX.X, op=ALU.max)
             sq_min = small.tile([P, NT], F32, name="sq_min")
-            nc.vector.tensor_tensor(out=sq_min[:], in0=st["x_min"][:], in1=st["k2"][:], op=ALU.add)
+            nc.vector.scalar_tensor_tensor(out=sq_min[:], in0=y_top[:], scalar=-2.0, in1=st["k2"][:],
+                                           op0=ALU.mult, op1=ALU.add)
             st["shift"] = small.tile([P, NT], F32, name="shift")
             nc.scalar.activation(out=st["shift"][:], in_=sq_min[:], func=ACT.Sqrt)
 
         def distances(b):
             step(lambda: keys_step(b))
             for i in range(NT):
-                step(lambda i=i: dist_step(b, i))
-            step(lambda: shift_step(b))
+                step(lambda i=i: dots(b, i), lambda i=i: root(b, i))
+            step(None, None, lambda: shift_step(b))
 
-        def tile_front(b, it, i):
+        def exponent(b, i):
             st = state[b]
-            if it == 0:
-                nc.scalar.activation(out=rows(b, i), in_=rows(b, i), func=ACT.Exp, bias=st["shift"][:, i:i + 1],
-                                     scale=-1.0, accum_out=st["s_first"][:, i:i + 1])
-                nc.vector.reciprocal(out=st["rho"][:, i:i + 1], in_=st["s_first"][:, i:i + 1])
-                nc.vector.tensor_scalar(out=rows(b, i), in0=rows(b, i), scalar1=st["rho"][:, i:i + 1],
-                                        scalar2=1.0 / N, op0=ALU.mult, op1=ALU.mult)
-            else:
-                junk = one.tile([P, T], BF16, name="junk", tag="j4")
-                nc.vector.scalar_tensor_tensor(
-                    out=junk[:], in0=rows(b, i), scalar=float(N), in1=st["w_all"][:],
-                    op0=ALU.mult, op1=ALU.mult, accum_out=st["s_n"][:, i:i + 1])
-                nc.vector.reciprocal(out=st["rho"][:, i:i + 1], in_=st["s_n"][:, i:i + 1])
-                nc.scalar.activation(out=rows(b, i), in_=rows(b, i), func=ACT.Copy,
-                                     scale=st["rho"][:, i:i + 1])
+            nc.scalar.activation(out=rows(b, i), in_=rows(b, i), func=ACT.Exp, bias=st["shift"][:, i:i + 1],
+                                 scale=-1.0, accum_out=st["s_first"][:, i:i + 1])
 
-        def tile_back(b, i):
+        def row_sum(b, i):
+            st = state[b]
+            junk = one.tile([P, T], BF16, name="junk", tag="j4")
+            nc.vector.scalar_tensor_tensor(
+                out=junk[:], in0=rows(b, i), scalar=float(N), in1=st["w_all"][:],
+                op0=ALU.mult, op1=ALU.mult, accum_out=st["s_n"][:, i:i + 1])
+
+        def invert(b, i, sums):
+            nc.vector.reciprocal(out=state[b]["rho"][:, i:i + 1], in_=state[b][sums][:, i:i + 1])
+
+        def scale_first(b, i):
+            nc.vector.tensor_scalar(out=rows(b, i), in0=rows(b, i), scalar1=state[b]["rho"][:, i:i + 1],
+                                    scalar2=1.0 / N, op0=ALU.mult, op1=ALU.mult)
+
+        def invert_scale(b, i):
+            invert(b, i, "s_n")
+            nc.scalar.activation(out=rows(b, i), in_=rows(b, i), func=ACT.Copy,
+                                 scale=state[b]["rho"][:, i:i + 1])
+
+        def column_sums(b, i):
             st = state[b]
             if i == 0:
                 st["acc"] = ps_a.tile([P, TT, P], F32, name="acc")
@@ -210,37 +219,56 @@ def tile_sinkhornattention_pa_t_kernel(tc, q_proj, k_proj, v, w_v, out):
                                  is_transpose=True,
                                  start=(i == 0 and a % 4 == 0), stop=(i == NT - 1 and a % 4 == 3))
             if i == NT - 1:
-                r_sum = small.tile([P, TT], F32, name="r_sum")
-                w_col = small.tile([P, TT], F32, name="w_col")
-                w_all = wide.tile([P, T], F32, name="w_all", tag="w8")
+                st["r_sum"] = small.tile([P, TT], F32, name="r_sum")
                 for g in range(4):
-                    nc.vector.tensor_reduce(out=r_sum[:, 4 * g:4 * g + 4], in_=st["acc"][:, 4 * g:4 * g + 4, :],
-                                            axis=AX.X, op=ALU.add)
-                    nc.vector.reciprocal(out=w_col[:, 4 * g:4 * g + 4], in_=r_sum[:, 4 * g:4 * g + 4])
-                spread(w_col, w_all)
-                st["w_all"] = w_all
+                    nc.vector.tensor_reduce(out=st["r_sum"][:, 4 * g:4 * g + 4],
+                                            in_=st["acc"][:, 4 * g:4 * g + 4, :], axis=AX.X, op=ALU.add)
+
+        def spread(b):
+            st = state[b]
+            w_col = small.tile([P, TT], F32, name="w_col")
+            nc.vector.reciprocal(out=w_col[:], in_=st["r_sum"][:])
+            w_all = wide.tile([P, T], F32, name="w_all", tag="w8")
+            for g in range(4):
+                pw = ps.tile([P, 512], F32, name="pw", tag="ps")
+                for a in range(4):
+                    nc.tensor.transpose(pw[:, a * P:(a + 1) * P],
+                                        w_col[:, 4 * g + a:4 * g + a + 1].to_broadcast([P, P]), ident_f[:])
+                nc.scalar.copy(out=w_all[:, g * 512:(g + 1) * 512], in_=pw[:])
+            st["w_all"] = w_all
 
         def sinkhorn_round(b, it):
             state[b]["rho"] = small.tile([P, NT], F32, name="rho")
-            state[b]["s_n"] = small.tile([P, NT], F32, name="s_n")
+            if it > 0:
+                state[b]["s_n"] = small.tile([P, NT], F32, name="s_n")
             for i in range(NT):
-                step(lambda i=i: tile_front(b, it, i), lambda i=i: tile_back(b, i))
+                last = (lambda: spread(b)) if i == NT - 1 else None
+                if it == 0:
+                    step(lambda i=i: exponent(b, i), lambda i=i: invert(b, i, "s_first"),
+                         lambda i=i: scale_first(b, i), None, lambda i=i: column_sums(b, i), last)
+                else:
+                    step(lambda i=i: row_sum(b, i), lambda i=i: invert_scale(b, i), None, None,
+                         lambda i=i: column_sums(b, i), last)
 
-        def plan_front(b, g, c):
+        def plan(b, g, c):
             st = state[b]
-            if c == 0:
-                st["codes", g] = wide.tile([P, 2, 512], U32, name="codes", tag="codes", align_bytes=64)
-                st["scales", g] = wide.tile([P, 2, 512], U8, name="scales", tag="scales", align_bytes=64)
             grp = wide.tile([P, 512, 4], BF16, name="grp", tag="g4", align_bytes=64)
             nc.vector.tensor_tensor(
                 out=grp[:],
                 in0=st["half"][c][:, :, g * 512:(g + 1) * 512].rearrange("p j t -> p t j"),
                 in1=st["w_all"][:, g * 512:(g + 1) * 512].unsqueeze(2).to_broadcast([P, 512, 4]),
                 op=ALU.mult)
-            nc.vector.quantize_mx(out=st["codes", g][:, c, :].bitcast(FP8X4), scales=st["scales", g][:, c, :],
-                                  in_=grp[:].rearrange("p t j -> p (t j)"))
+            st["grp", g, c] = grp
 
-        def plan_back(b, g):
+        def quantise(b, g, c):
+            st = state[b]
+            if c == 0:
+                st["codes", g] = wide.tile([P, 2, 512], U32, name="codes", tag="codes", align_bytes=64)
+                st["scales", g] = wide.tile([P, 2, 512], U8, name="scales", tag="scales", align_bytes=64)
+            nc.vector.quantize_mx(out=st["codes", g][:, c, :].bitcast(FP8X4), scales=st["scales", g][:, c, :],
+                                  in_=st["grp", g, c][:].rearrange("p t j -> p (t j)"))
+
+        def multiply(b, g):
             codes = state[b]["codes", g]
             scales = state[b]["scales", g]
             po = ps.tile([P, 4, D], F32, name="po", tag="ps")
@@ -258,8 +286,8 @@ def tile_sinkhornattention_pa_t_kernel(tc, q_proj, k_proj, v, w_v, out):
 
         def attend(b):
             for g in range(4):
-                step(lambda g=g: plan_front(b, g, 0))
-                step(lambda g=g: plan_front(b, g, 1), lambda g=g: plan_back(b, g))
+                step(lambda g=g: plan(b, g, 0), lambda g=g: quantise(b, g, 0))
+                step(lambda g=g: plan(b, g, 1), lambda g=g: quantise(b, g, 1), lambda g=g: multiply(b, g))
 
         for first in range(0, B, 2):
             pair = (first, first + 1)
@@ -267,12 +295,11 @@ def tile_sinkhornattention_pa_t_kernel(tc, q_proj, k_proj, v, w_v, out):
                 if first > 0:
                     attend(b - 2)
                 distances(b)
-            if first == 0:
-                value_projection()
+            value_projection(pair)
             for it in range(ITERS):
                 for b in pair:
                     sinkhorn_round(b, it)
         for b in (B - 2, B - 1):
             attend(b)
-        for n in range(LAG):
-            step(lambda: None)
+        while pending:
+            step()

@@ -30,6 +30,7 @@ def tile_sinkhornattention_pa_t_kernel(tc, q_proj, k_proj, v, w_v, out):
         small = ctx.enter_context(tc.tile_pool(name="small", bufs=4))
         wide = ctx.enter_context(tc.tile_pool(name="wide", bufs=2))
         one = ctx.enter_context(tc.tile_pool(name="one", bufs=1))
+        scrap = ctx.enter_context(tc.tile_pool(name="scrap", bufs=3))
         ps_a = ctx.enter_context(tc.psum_pool(name="ps_a", bufs=1))
         ps = ctx.enter_context(tc.psum_pool(name="ps", bufs=4))
 
@@ -193,7 +194,7 @@ def tile_sinkhornattention_pa_t_kernel(tc, q_proj, k_proj, v, w_v, out):
 
         def row_sum(b, i):
             st = state[b]
-            junk = one.tile([P, T], BF16, name="junk", tag="j4")
+            junk = scrap.tile([P, T], BF16, name="junk")
             nc.vector.scalar_tensor_tensor(
                 out=junk[:], in0=rows(b, i), scalar=float(N), in1=st["w_all"][:],
                 op0=ALU.mult, op1=ALU.mult, accum_out=st["s_n"][:, i:i + 1])

@@ -26,7 +26,7 @@ def tile_sinkhornattention_pa_t_kernel(tc, q_proj, k_proj, v, w_v, out):
         ctx.enter_context(tc.manual_schedule())
         const = ctx.enter_context(tc.tile_pool(name="const", bufs=1))
         kern = ctx.enter_context(tc.tile_pool(name="kern", bufs=4))
-        keys = ctx.enter_context(tc.tile_pool(name="keys", bufs=2))
+        group = ctx.enter_context(tc.tile_pool(name="group", bufs=3))
         small = ctx.enter_context(tc.tile_pool(name="small", bufs=4))
         wide = ctx.enter_context(tc.tile_pool(name="wide", bufs=2))
         one = ctx.enter_context(tc.tile_pool(name="one", bufs=1))
@@ -40,6 +40,9 @@ def tile_sinkhornattention_pa_t_kernel(tc, q_proj, k_proj, v, w_v, out):
         make_identity(nc, ident_b[:])
         q_t = const.tile([P, T], BF16, name="q_t")
         nq2h = const.tile([P, TT], F32, name="nq2h")
+        k_t = const.tile([P, B, NT, P], BF16, name="k_t")
+        k2 = const.tile([P, B, NT], F32, name="k2")
+        k2h = const.tile([P, B, NT], F32, name="k2h")
         vp_codes = const.tile([P, B, 2, P], U32, name="vp_codes", align_bytes=64)
         vp_scales = const.tile([P, B, 2, P], U8, name="vp_scales", align_bytes=64)
         wv_codes = const.tile([P, D], U32, name="wv_codes", align_bytes=64)
@@ -93,7 +96,7 @@ def tile_sinkhornattention_pa_t_kernel(tc, q_proj, k_proj, v, w_v, out):
                 nc.sync.dma_start(out=v_new[:], in_=v[b].rearrange("(c p j) f -> p c j f", c=2, j=4))
                 state[b]["v_sb"] = v_new
             v_sb = state[b]["v_sb"]
-            v_grp = wide.tile([P, 4 * P * 4], BF16, name="v_grp", tag="g4", align_bytes=64)
+            v_grp = group.tile([P, 4 * P * 4], BF16, name="v_grp", tag="g4", align_bytes=64)
             v_words = v_grp[:].bitcast(F32).rearrange("q (j n u) -> q j n u", j=4, u=2)
             for h in range(2):
                 pv = ps.tile([P, 2, 2, P], F32, name="pv", tag="ps")
@@ -128,35 +131,29 @@ def tile_sinkhornattention_pa_t_kernel(tc, q_proj, k_proj, v, w_v, out):
                 for c in range(2):
                     step(lambda b=b, c=c: vp_step(b, c))
 
-        def keys_step(b):
-            st = state[b]
-            k_sb = k_all[:, b, :, :]
-            k_sq = one.tile([P, NT, D], F32, name="k_sq")
-            nc.vector.tensor_tensor(out=k_sq[:], in0=k_sb, in1=k_sb, op=ALU.mult)
-            k2 = small.tile([P, NT], F32, name="k2")
-            nc.vector.tensor_reduce(out=k2[:], in_=k_sq[:], axis=AX.X, op=ALU.add)
-            k_t = keys.tile([P, NT, P], BF16, name="k_t")
+        def prepare_keys(b):
+            for i in range(NT):
+                drop = small.tile([P, D], F32, name="drop")
+                nc.scalar.activation(out=drop[:], in_=k_all[:, b, i, :], func=ACT.Square,
+                                     accum_out=k2[:, b, i:i + 1])
+            nc.scalar.activation(out=k2h[:, b, :], in_=k2[:, b, :], func=ACT.Copy, scale=0.5)
             for g in range(2):
                 pk = ps.tile([P, 4, P], BF16, name="pk", tag="ps")
                 for a in range(4):
-                    nc.tensor.transpose(pk[:, a, :], k_sb[:, 4 * g + a, :], ident_b[:])
-                nc.vector.tensor_copy(out=k_t[:, 4 * g:4 * g + 4, :], in_=pk[:])
-            k2h = small.tile([P, NT], F32, name="k2h")
-            nc.vector.tensor_scalar(out=k2h[:], in0=k2[:], scalar1=0.5, scalar2=None, op0=ALU.mult)
-            st["k2"] = k2
-            st["k2h"] = k2h
-            st["k_t"] = k_t
-            st["half"] = []
-            st["y_max"] = small.tile([P, NT, 4], F32, name="y_max")
-            st["s_first"] = small.tile([P, NT], F32, name="s_first")
+                    nc.tensor.transpose(pk[:, a, :], k_all[:, b, 4 * g + a, :], ident_b[:])
+                nc.vector.tensor_copy(out=k_t[:, b, 4 * g:4 * g + 4, :], in_=pk[:])
 
         def dots(b, i):
             st = state[b]
+            if i == 0:
+                st["half"] = []
+                st["y_max"] = small.tile([P, NT, 4], F32, name="y_max")
+                st["s_first"] = small.tile([P, NT], F32, name="s_first")
             if i % 4 == 0:
                 st["half"].append(kern.tile([P, 4, T], F32, name="half", tag="half"))
             for ch in range(4):
                 pd = ps.tile([P, 512], F32, name="pd", tag="ps")
-                nc.tensor.matmul(pd[:], lhsT=st["k_t"][:, i, :], rhs=q_t[:, ch * 512:(ch + 1) * 512],
+                nc.tensor.matmul(pd[:], lhsT=k_t[:, b, i, :], rhs=q_t[:, ch * 512:(ch + 1) * 512],
                                  start=True, stop=False)
                 for a in range(4):
                     col = 4 * ch + a
@@ -164,11 +161,11 @@ def tile_sinkhornattention_pa_t_kernel(tc, q_proj, k_proj, v, w_v, out):
                                      lhsT=nq2h[:, col:col + 1].to_broadcast([P, P]), rhs=ident_f[:],
                                      is_transpose=True, start=False, stop=(a == 3))
                 nc.vector.tensor_scalar(out=rows(b, i)[:, ch * 512:(ch + 1) * 512], in0=pd[:],
-                                        scalar1=st["k2h"][:, i:i + 1], scalar2=None,
+                                        scalar1=k2h[:, b, i:i + 1], scalar2=None,
                                         op0=ALU.min, op1=ALU.max, accum_out=st["y_max"][:, i, ch:ch + 1])
 
         def root(b, i):
-            nc.scalar.activation(out=rows(b, i), in_=rows(b, i), func=ACT.Sqrt, bias=state[b]["k2"][:, i:i + 1],
+            nc.scalar.activation(out=rows(b, i), in_=rows(b, i), func=ACT.Sqrt, bias=k2[:, b, i:i + 1],
                                  scale=-2.0)
 
         def shift_step(b):
@@ -176,13 +173,12 @@ def tile_sinkhornattention_pa_t_kernel(tc, q_proj, k_proj, v, w_v, out):
             y_top = small.tile([P, NT], F32, name="y_top")
             nc.vector.tensor_reduce(out=y_top[:], in_=st["y_max"][:], axis=AX.X, op=ALU.max)
             sq_min = small.tile([P, NT], F32, name="sq_min")
-            nc.vector.scalar_tensor_tensor(out=sq_min[:], in0=y_top[:], scalar=-2.0, in1=st["k2"][:],
+            nc.vector.scalar_tensor_tensor(out=sq_min[:], in0=y_top[:], scalar=-2.0, in1=k2[:, b, :],
                                            op0=ALU.mult, op1=ALU.add)
             st["shift"] = small.tile([P, NT], F32, name="shift")
             nc.scalar.activation(out=st["shift"][:], in_=sq_min[:], func=ACT.Sqrt)
 
         def distances(b):
-            step(lambda: keys_step(b))
             for i in range(NT):
                 step(lambda i=i: dots(b, i), lambda i=i: root(b, i))
             step(None, None, lambda: shift_step(b))
@@ -253,7 +249,7 @@ def tile_sinkhornattention_pa_t_kernel(tc, q_proj, k_proj, v, w_v, out):
 
         def plan(b, g, c):
             st = state[b]
-            grp = wide.tile([P, 512, 4], BF16, name="grp", tag="g4", align_bytes=64)
+            grp = group.tile([P, 512, 4], BF16, name="grp", tag="g4", align_bytes=64)
             nc.vector.tensor_tensor(
                 out=grp[:],
                 in0=st["half"][c][:, :, g * 512:(g + 1) * 512].rearrange("p j t -> p t j"),
@@ -290,12 +286,16 @@ def tile_sinkhornattention_pa_t_kernel(tc, q_proj, k_proj, v, w_v, out):
                 step(lambda g=g: plan(b, g, 0), lambda g=g: quantise(b, g, 0))
                 step(lambda g=g: plan(b, g, 1), lambda g=g: quantise(b, g, 1), lambda g=g: multiply(b, g))
 
+        prepare_keys(0)
+        prepare_keys(1)
         for first in range(0, B, 2):
             pair = (first, first + 1)
             for b in pair:
                 if first > 0:
                     attend(b - 2)
                 distances(b)
+                if b + 2 < B:
+                    step(lambda b=b: prepare_keys(b + 2))
             value_projection(pair)
             for it in range(ITERS):
                 for b in pair:

@@ -251,9 +251,10 @@ def tile_sinkhornattention_pa_t_kernel(tc, q_proj, k_proj, v, w_v, out):
             st = state[b]
             grp = group.tile([P, 512, 4], BF16, name="grp", tag="g4", align_bytes=64)
             nc.vector.tensor_tensor(
-                out=grp[:],
-                in0=st["half"][c][:, :, g * 512:(g + 1) * 512].rearrange("p j t -> p t j"),
-                in1=st["w_all"][:, g * 512:(g + 1) * 512].unsqueeze(2).to_broadcast([P, 512, 4]),
+                out=grp[:].rearrange("p (r i) j -> p r j i", i=4),
+                in0=st["half"][c][:, :, g * 512:(g + 1) * 512].rearrange("p j (r i) -> p r j i", i=4),
+                in1=st["w_all"][:, g * 512:(g + 1) * 512].rearrange("p (r i) -> p r i", i=4)
+                .unsqueeze(2).to_broadcast([P, 128, 4, 4]),
                 op=ALU.mult)
             st["grp", g, c] = grp
 

@@ -151,18 +151,22 @@ def tile_sinkhornattention_pa_t_kernel(tc, q_proj, k_proj, v, w_v, out):
                 st["s_first"] = small.tile([P, NT], F32, name="s_first")
             if i % 4 == 0:
                 st["half"].append(kern.tile([P, 4, T], F32, name="half", tag="half"))
-            for ch in range(4):
-                pd = ps.tile([P, 512], F32, name="pd", tag="ps")
-                nc.tensor.matmul(pd[:], lhsT=k_t[:, b, i, :], rhs=q_t[:, ch * 512:(ch + 1) * 512],
-                                 start=True, stop=False)
-                for a in range(4):
-                    col = 4 * ch + a
-                    nc.tensor.matmul(pd[:, a * P:(a + 1) * P],
-                                     lhsT=nq2h[:, col:col + 1].to_broadcast([P, P]), rhs=ident_f[:],
-                                     is_transpose=True, start=False, stop=(a == 3))
-                nc.vector.tensor_scalar(out=rows(b, i)[:, ch * 512:(ch + 1) * 512], in0=pd[:],
-                                        scalar1=k2h[:, b, i:i + 1], scalar2=None,
-                                        op0=ALU.min, op1=ALU.max, accum_out=st["y_max"][:, i, ch:ch + 1])
+            for pair_ch in ((0, 1), (2, 3)):
+                banks = {}
+                for ch in pair_ch:
+                    pd = ps.tile([P, 512], F32, name="pd", tag="ps")
+                    nc.tensor.matmul(pd[:], lhsT=k_t[:, b, i, :], rhs=q_t[:, ch * 512:(ch + 1) * 512],
+                                     start=True, stop=False)
+                    banks[ch] = pd
+                for ch in pair_ch:
+                    for a in range(4):
+                        col = 4 * ch + a
+                        nc.tensor.matmul(banks[ch][:, a * P:(a + 1) * P],
+                                         lhsT=nq2h[:, col:col + 1].to_broadcast([P, P]), rhs=ident_f[:],
+                                         is_transpose=True, start=False, stop=(a == 3))
+                    nc.vector.tensor_scalar(out=rows(b, i)[:, ch * 512:(ch + 1) * 512], in0=banks[ch][:],
+                                            scalar1=k2h[:, b, i:i + 1], scalar2=None,
+                                            op0=ALU.min, op1=ALU.max, accum_out=st["y_max"][:, i, ch:ch + 1])
 
         def root(b, i):
             nc.scalar.activation(out=rows(b, i), in_=rows(b, i), func=ACT.Sqrt, bias=k2[:, b, i:i + 1],

@@ -17,6 +17,8 @@ ITERS = 5
 P = 128
 NT = N // P
 TT = T // P
+FIRST_TICK = 5
+MID_BLOCKS, TAIL_BLOCKS = 3, 4
 FLOPS = 2 * B * (2 * T * N * D + N * VD * D)
 
 
@@ -26,12 +28,13 @@ def tile_sinkhornattention_pa_t_kernel(tc, q_proj, k_proj, v, w_v, out):
         ctx.enter_context(tc.manual_schedule())
         const = ctx.enter_context(tc.tile_pool(name="const", bufs=1))
         kern = ctx.enter_context(tc.tile_pool(name="kern", bufs=4))
-        group = ctx.enter_context(tc.tile_pool(name="group", bufs=3))
+        group = ctx.enter_context(tc.tile_pool(name="group", bufs=4))
+        mids = ctx.enter_context(tc.tile_pool(name="mids", bufs=3))
         small = ctx.enter_context(tc.tile_pool(name="small", bufs=4))
         wide = ctx.enter_context(tc.tile_pool(name="wide", bufs=2))
         one = ctx.enter_context(tc.tile_pool(name="one", bufs=1))
         scrap = ctx.enter_context(tc.tile_pool(name="scrap", bufs=3))
-        ps_a = ctx.enter_context(tc.psum_pool(name="ps_a", bufs=1))
+        ps_a = ctx.enter_context(tc.psum_pool(name="ps_a", bufs=4))
         ps = ctx.enter_context(tc.psum_pool(name="ps", bufs=4))
 
         ident_f = const.tile([P, P], F32, name="ident_f")
@@ -60,10 +63,15 @@ def tile_sinkhornattention_pa_t_kernel(tc, q_proj, k_proj, v, w_v, out):
             for part in reversed(pending.pop(0)):
                 part()
 
+        def later(part):
+            if not pending:
+                pending.append([])
+            pending[0].append(part)
+
         def rows(b, i):
             return state[b]["half"][i // 4][:, i % 4, :]
 
-        q_sb = one.tile([P, TT, D], BF16, name="q_sb", tag="j4")
+        q_sb = group.tile([P, TT, D], BF16, name="q_sb", tag="g4", align_bytes=64)
         nc.sync.dma_start(out=q_sb[:], in_=q_proj.rearrange("(p a) d -> p a d", a=TT))
         k_all = const.tile([P, B, NT, D], BF16, name="k_all")
         for b in range(B):
@@ -182,10 +190,19 @@ def tile_sinkhornattention_pa_t_kernel(tc, q_proj, k_proj, v, w_v, out):
             st["shift"] = small.tile([P, NT], F32, name="shift")
             nc.scalar.activation(out=st["shift"][:], in_=sq_min[:], func=ACT.Sqrt)
 
-        def distances(b):
+        def distances(b, before=None, stream=(), mine=()):
+
+            def beside(i):
+                for tick in stream[2 * i:2 * i + 2]:
+                    tick()
+                if i % 2 == 1 and i // 2 < len(mine):
+                    plan_step(before, *mine[i // 2])
+
             for i in range(NT):
-                step(lambda i=i: dots(b, i), lambda i=i: root(b, i))
+                step(lambda i=i: (dots(b, i), beside(i)), lambda i=i: root(b, i))
             step(None, None, lambda: shift_step(b))
+            for block in mine[NT // 2:]:
+                step(lambda block=block: plan_step(before, *block))
 
         def exponent(b, i):
             st = state[b]
@@ -214,20 +231,22 @@ def tile_sinkhornattention_pa_t_kernel(tc, q_proj, k_proj, v, w_v, out):
         def column_sums(b, i):
             st = state[b]
             if i == 0:
-                st["acc"] = ps_a.tile([P, TT, P], F32, name="acc")
+                for g in range(4):
+                    st["acc", g] = ps_a.tile([P, 4, P], F32, name="acc", tag="acc")
             for a in range(TT):
-                nc.tensor.matmul(st["acc"][:, a, :], lhsT=rows(b, i)[:, a * P:(a + 1) * P], rhs=ident_f[:],
+                nc.tensor.matmul(st["acc", a // 4][:, a % 4, :], lhsT=rows(b, i)[:, a * P:(a + 1) * P], rhs=ident_f[:],
                                  is_transpose=True,
                                  start=(i == 0 and a % 4 == 0), stop=(i == NT - 1 and a % 4 == 3))
             if i == NT - 1:
                 st["r_sum"] = small.tile([P, TT], F32, name="r_sum")
                 for g in range(4):
                     nc.vector.tensor_reduce(out=st["r_sum"][:, 4 * g:4 * g + 4],
-                                            in_=st["acc"][:, 4 * g:4 * g + 4, :], axis=AX.X, op=ALU.add)
+                                            in_=st["acc", g][:], axis=AX.X, op=ALU.add)
 
         def spread(b):
             st = state[b]
             w_col = small.tile([P, TT], F32, name="w_col")
+            st["w_col"] = w_col
             nc.vector.reciprocal(out=w_col[:], in_=st["r_sum"][:])
             w_all = wide.tile([P, T], F32, name="w_all", tag="w8")
             for g in range(4):
@@ -248,8 +267,10 @@ def tile_sinkhornattention_pa_t_kernel(tc, q_proj, k_proj, v, w_v, out):
                     step(lambda i=i: exponent(b, i), lambda i=i: invert(b, i, "s_first"),
                          lambda i=i: scale_first(b, i), None, lambda i=i: column_sums(b, i), last)
                 else:
+                    hurry = it == ITERS - 1 and b % 2 == 1 and i == NT - 1
                     step(lambda i=i: row_sum(b, i), lambda i=i: invert_scale(b, i), None, None,
-                         lambda i=i: column_sums(b, i), last)
+                         lambda i=i, hurry=hurry: (column_sums(b, i), spread(b) if hurry else None),
+                         None if hurry else last)
 
         def plan(b, g, c):
             st = state[b]
@@ -264,7 +285,7 @@ def tile_sinkhornattention_pa_t_kernel(tc, q_proj, k_proj, v, w_v, out):
 
         def quantise(b, g, c):
             st = state[b]
-            if c == 0:
+            if ("codes", g) not in st:
                 st["codes", g] = wide.tile([P, 2, 512], U32, name="codes", tag="codes", align_bytes=64)
                 st["scales", g] = wide.tile([P, 2, 512], U8, name="scales", tag="scales", align_bytes=64)
             nc.vector.quantize_mx(out=st["codes", g][:, c, :].bitcast(FP8X4), scales=st["scales", g][:, c, :],
@@ -286,26 +307,84 @@ def tile_sinkhornattention_pa_t_kernel(tc, q_proj, k_proj, v, w_v, out):
             nc.scalar.copy(out=o_sb[:], in_=po[:])
             nc.sync.dma_start(out=out[b].rearrange("(p a) d -> p a d", a=TT)[:, 4 * g:4 * g + 4, :], in_=o_sb[:])
 
-        def attend(b):
-            for g in range(4):
-                step(lambda g=g: plan(b, g, 0), lambda g=g: quantise(b, g, 0))
-                step(lambda g=g: plan(b, g, 1), lambda g=g: quantise(b, g, 1), lambda g=g: multiply(b, g))
+        def code(b, g, c):
+            quantise(b, g, c)
+            state[b]["coded", g] = state[b].get(("coded", g), 0) + 1
+            if state[b]["coded", g] == 2:
+                later(lambda: multiply(b, g))
+
+        def plan_step(b, g, c):
+            plan(b, g, c)
+            later(lambda: code(b, g, c))
+
+        def turn(b, g, a):
+            st = state[b]
+            if a == 0:
+                st["grp", g, 1] = group.tile([P, 512, 4], BF16, name="grp", tag="g4", align_bytes=64)
+            st["turned"] = ps_a.tile([P, 4, P], F32, name="turned", tag="acc")
+            cols = slice(g * 512 + a * P, g * 512 + (a + 1) * P)
+            for j in range(4):
+                nc.tensor.transpose(st["turned"][:, j, :], st["half"][1][:, j, cols], ident_f[:])
+
+        def weigh(b, g, a):
+            st = state[b]
+            st["mid", a] = mids.tile([P, 4, P], F32, name="mid")
+            nc.scalar.activation(out=st["mid", a][:], in_=st["turned"][:], func=ACT.Copy,
+                                 scale=st["w_col"][:, 4 * g + a:4 * g + a + 1])
+
+        def turn_back(b, g, a):
+            st = state[b]
+            back = ps_a.tile([P, 4, P], F32, name="back", tag="acc")
+            for j in range(4):
+                nc.tensor.transpose(back[:, j, :], st["mid", a][:, j, :], ident_f[:])
+            nc.scalar.copy(out=st["grp", g, 1][:, a * P:(a + 1) * P, :], in_=back[:].rearrange("p j t -> p t j"))
+            if a == 3:
+                later(lambda: code(b, g, 1))
+
+        def ticks(b, s_blocks):
+            units = [(g, a) for g in range(s_blocks) for a in range(4)]
+
+            def tick(u):
+                if 0 <= u - 1 < len(units):
+                    weigh(b, *units[u - 1])
+                if u < len(units):
+                    turn(b, *units[u])
+                if 0 <= u - 2 < len(units):
+                    turn_back(b, *units[u - 2])
+            return [lambda u=u: tick(u) for u in range(len(units) + 2)]
+
+        def blocks(s_blocks):
+            return [(g, 0) for g in range(4)] + [(g, 1) for g in range(s_blocks, 4)]
+
+        def attend(b, stream=(), first_tick=0):
+            stream = list(stream)
+            for s in range(8):
+                mine = stream[:2] if s >= first_tick else []
+                stream = stream[len(mine):]
+                step(lambda s=s, mine=mine: (plan_step(b, s // 2, s % 2), [tick() for tick in mine]))
+            return stream
 
         prepare_keys(0)
         prepare_keys(1)
         for first in range(0, B, 2):
             pair = (first, first + 1)
             for b in pair:
-                if first > 0:
-                    attend(b - 2)
-                distances(b)
+                if first > 0 and b == first:
+                    rest = attend(b - 2, ticks(b - 1, MID_BLOCKS), FIRST_TICK)
+                    distances(b, b - 1, rest, blocks(MID_BLOCKS))
+                else:
+                    distances(b)
                 if b + 2 < B:
                     step(lambda b=b: prepare_keys(b + 2))
             value_projection(pair)
             for it in range(ITERS):
                 for b in pair:
                     sinkhorn_round(b, it)
-        for b in (B - 2, B - 1):
-            attend(b)
+        rest = attend(B - 2, ticks(B - 1, TAIL_BLOCKS), FIRST_TICK)
+        for block in blocks(TAIL_BLOCKS):
+            step(lambda block=block, mine=rest[:2]: (plan_step(B - 1, *block), [tick() for tick in mine]))
+            rest = rest[2:]
+        for tick in rest:
+            step(tick)
         while pending:
             step()

@@ -17,6 +17,7 @@ ITERS = 5
 P = 128
 NT = N // P
 TT = T // P
+V_BANKS = 3
 FIRST_TICK = 5
 MID_BLOCKS, TAIL_BLOCKS = 3, 4
 FLOPS = 2 * B * (2 * T * N * D + N * VD * D)
@@ -43,6 +44,8 @@ def tile_sinkhornattention_pa_t_kernel(tc, q_proj, k_proj, v, w_v, out):
         make_identity(nc, ident_b[:])
         q_t = const.tile([P, T], BF16, name="q_t")
         nq2h = const.tile([P, TT], F32, name="nq2h")
+        w_cols = const.tile([P, B, 32], F32, name="w_cols", align_bytes=64)
+        nc.gpsimd.memset(w_cols[:], 1.0)
         k_t = const.tile([P, B, NT, P], BF16, name="k_t")
         k2 = const.tile([P, B, NT], F32, name="k2")
         k2h = const.tile([P, B, NT], F32, name="k2h")
@@ -72,7 +75,8 @@ def tile_sinkhornattention_pa_t_kernel(tc, q_proj, k_proj, v, w_v, out):
             return state[b]["half"][i // 4][:, i % 4, :]
 
         q_sb = group.tile([P, TT, D], BF16, name="q_sb", tag="g4", align_bytes=64)
-        nc.sync.dma_start(out=q_sb[:], in_=q_proj.rearrange("(p a) d -> p a d", a=TT))
+        for g in range(0, TT, 8):
+            nc.sync.dma_start(out=q_sb[:, g:g + 8, :], in_=q_proj.rearrange("(p a) d -> p a d", a=TT)[:, g:g + 8, :])
         k_all = const.tile([P, B, NT, D], BF16, name="k_all")
         for b in range(B):
             nc.sync.dma_start(
@@ -83,11 +87,16 @@ def tile_sinkhornattention_pa_t_kernel(tc, q_proj, k_proj, v, w_v, out):
             for a in range(4):
                 nc.tensor.transpose(pt[:, a * P:(a + 1) * P], q_sb[:, 4 * g + a, :], ident_b[:])
             nc.vector.tensor_copy(out=q_t[:, g * 512:(g + 1) * 512], in_=pt[:])
-        q_sq = wide.tile([P, TT, D], F32, name="q_sq", tag="w8")
-        nc.vector.tensor_tensor(out=q_sq[:], in0=q_sb[:], in1=q_sb[:], op=ALU.mult)
         q2 = small.tile([P, TT], F32, name="q2")
-        nc.vector.tensor_reduce(out=q2[:], in_=q_sq[:], axis=AX.X, op=ALU.add)
-        nc.vector.tensor_scalar(out=nq2h[:], in0=q2[:], scalar1=-0.5, scalar2=None, op0=ALU.mult)
+        for a in range(TT):
+            drop = small.tile([P, D], F32, name="drop")
+            nc.scalar.activation(out=drop[:], in_=q_sb[:, a, :], func=ACT.Square, accum_out=q2[:, a:a + 1])
+            if a % 4 == 3:
+                nc.scalar.activation(out=nq2h[:, a - 3:a + 1], in_=q2[:, a - 3:a + 1], func=ACT.Copy, scale=-0.5)
+        k_sq = wide.tile([P, NT, D], F32, name="k_sq", tag="w8")
+        nc.vector.tensor_tensor(out=k_sq[:], in0=k_all[:, 0, :, :], in1=k_all[:, 0, :, :], op=ALU.mult)
+        nc.vector.tensor_reduce(out=k2[:, 0, :], in_=k_sq[:], axis=AX.X, op=ALU.add)
+        nc.vector.tensor_scalar(out=k2h[:, 0, :], in0=k2[:, 0, :], scalar1=0.5, scalar2=None, op0=ALU.mult)
 
         def wv_step():
             wv_sb = one.tile([P, 2, 2, D], BF16, name="wv_sb")
@@ -139,12 +148,14 @@ def tile_sinkhornattention_pa_t_kernel(tc, q_proj, k_proj, v, w_v, out):
                 for c in range(2):
                     step(lambda b=b, c=c: vp_step(b, c))
 
-        def prepare_keys(b):
+        def square_keys(b):
             for i in range(NT):
                 drop = small.tile([P, D], F32, name="drop")
                 nc.scalar.activation(out=drop[:], in_=k_all[:, b, i, :], func=ACT.Square,
                                      accum_out=k2[:, b, i:i + 1])
             nc.scalar.activation(out=k2h[:, b, :], in_=k2[:, b, :], func=ACT.Copy, scale=0.5)
+
+        def turn_keys(b):
             for g in range(2):
                 pk = ps.tile([P, 4, P], BF16, name="pk", tag="ps")
                 for a in range(4):
@@ -193,6 +204,9 @@ def tile_sinkhornattention_pa_t_kernel(tc, q_proj, k_proj, v, w_v, out):
         def distances(b, before=None, stream=(), mine=()):
 
             def beside(i):
+                if i == 3 and b + 1 < B:
+                    square_keys(b + 1)
+                    turn_keys(b + 1)
                 for tick in stream[2 * i:2 * i + 2]:
                     tick()
                 if i % 2 == 1 and i // 2 < len(mine):
@@ -239,36 +253,38 @@ def tile_sinkhornattention_pa_t_kernel(tc, q_proj, k_proj, v, w_v, out):
                                  start=(i == 0 and a % 4 == 0), stop=(i == NT - 1 and a % 4 == 3))
             if i == NT - 1:
                 st["r_sum"] = small.tile([P, TT], F32, name="r_sum")
-                for g in range(4):
+                for g in range(V_BANKS):
                     nc.vector.tensor_reduce(out=st["r_sum"][:, 4 * g:4 * g + 4],
                                             in_=st["acc", g][:], axis=AX.X, op=ALU.add)
+                for a in range(4 * V_BANKS, TT):
+                    drop = small.tile([P, D], F32, name="drop")
+                    nc.scalar.activation(out=drop[:], in_=st["acc", a // 4][:, a % 4, :], func=ACT.Copy,
+                                         accum_out=st["r_sum"][:, a:a + 1])
 
         def spread(b):
             st = state[b]
-            w_col = small.tile([P, TT], F32, name="w_col")
-            st["w_col"] = w_col
-            nc.vector.reciprocal(out=w_col[:], in_=st["r_sum"][:])
-            w_all = wide.tile([P, T], F32, name="w_all", tag="w8")
-            for g in range(4):
-                pw = ps.tile([P, 512], F32, name="pw", tag="ps")
-                for a in range(4):
-                    nc.tensor.transpose(pw[:, a * P:(a + 1) * P],
-                                        w_col[:, 4 * g + a:4 * g + a + 1].to_broadcast([P, P]), ident_f[:])
-                nc.scalar.copy(out=w_all[:, g * 512:(g + 1) * 512], in_=pw[:])
-            st["w_all"] = w_all
+            nc.vector.reciprocal(out=w_cols[:, b, 0:TT], in_=st["r_sum"][:])
+            w_turn = small.tile([P, 32], F32, name="w_turn", align_bytes=64)
+            nc.vector.transpose(out=w_turn[:], in_=w_cols[:, b, :])
+            corner = out[b, st["round"] * TT:(st["round"] + 1) * TT, :]
+            for quad in range(0, P, 32):
+                nc.sync.dma_start(out=corner[:, quad:quad + 32], in_=w_turn[quad:quad + TT, :])
+            st["w_all"] = wide.tile([P, T], F32, name="w_all", tag="w8")
+            nc.sync.dma_start(out=st["w_all"][:], in_=corner.rearrange("a p -> (a p)").partition_broadcast(P))
 
         def sinkhorn_round(b, it):
             state[b]["rho"] = small.tile([P, NT], F32, name="rho")
+            state[b]["round"] = it
             if it > 0:
                 state[b]["s_n"] = small.tile([P, NT], F32, name="s_n")
             for i in range(NT):
                 last = (lambda: spread(b)) if i == NT - 1 else None
                 if it == 0:
                     step(lambda i=i: exponent(b, i), lambda i=i: invert(b, i, "s_first"),
-                         lambda i=i: scale_first(b, i), None, lambda i=i: column_sums(b, i), last)
+                         lambda i=i: scale_first(b, i), lambda i=i: column_sums(b, i), last)
                 else:
                     hurry = it == ITERS - 1 and b % 2 == 1 and i == NT - 1
-                    step(lambda i=i: row_sum(b, i), lambda i=i: invert_scale(b, i), None, None,
+                    step(lambda i=i: row_sum(b, i), lambda i=i: invert_scale(b, i), None,
                          lambda i=i, hurry=hurry: (column_sums(b, i), spread(b) if hurry else None),
                          None if hurry else last)
 
@@ -330,7 +346,7 @@ def tile_sinkhornattention_pa_t_kernel(tc, q_proj, k_proj, v, w_v, out):
             st = state[b]
             st["mid", a] = mids.tile([P, 4, P], F32, name="mid")
             nc.scalar.activation(out=st["mid", a][:], in_=st["turned"][:], func=ACT.Copy,
-                                 scale=st["w_col"][:, 4 * g + a:4 * g + a + 1])
+                                 scale=w_cols[:, b, 4 * g + a:4 * g + a + 1])
 
         def turn_back(b, g, a):
             st = state[b]
@@ -364,8 +380,7 @@ def tile_sinkhornattention_pa_t_kernel(tc, q_proj, k_proj, v, w_v, out):
                 step(lambda s=s, mine=mine: (plan_step(b, s // 2, s % 2), [tick() for tick in mine]))
             return stream
 
-        prepare_keys(0)
-        prepare_keys(1)
+        turn_keys(0)
         for first in range(0, B, 2):
             pair = (first, first + 1)
             for b in pair:
@@ -374,8 +389,6 @@ def tile_sinkhornattention_pa_t_kernel(tc, q_proj, k_proj, v, w_v, out):
                     distances(b, b - 1, rest, blocks(MID_BLOCKS))
                 else:
                     distances(b)
-                if b + 2 < B:
-                    step(lambda b=b: prepare_keys(b + 2))
             value_projection(pair)
             for it in range(ITERS):
                 for b in pair:

@@ -18,7 +18,8 @@ P = 128
 NT = N // P
 TT = T // P
 V_BANKS = 3
-FIRST_TICK = 5
+ORDER = ((0, 1), (1, 1), (2, 1), (3, 1), (3, 0), (2, 0), (1, 0), (0, 0))
+FIRST_TICK = 3
 MID_BLOCKS, TAIL_BLOCKS = 3, 4
 FLOPS = 2 * B * (2 * T * N * D + N * VD * D)
 
@@ -34,6 +35,7 @@ def tile_sinkhornattention_pa_t_kernel(tc, q_proj, k_proj, v, w_v, out):
         small = ctx.enter_context(tc.tile_pool(name="small", bufs=4))
         wide = ctx.enter_context(tc.tile_pool(name="wide", bufs=2))
         one = ctx.enter_context(tc.tile_pool(name="one", bufs=1))
+        coded = ctx.enter_context(tc.tile_pool(name="coded", bufs=3))
         scrap = ctx.enter_context(tc.tile_pool(name="scrap", bufs=3))
         ps_a = ctx.enter_context(tc.psum_pool(name="ps_a", bufs=4))
         ps = ctx.enter_context(tc.psum_pool(name="ps", bufs=4))
@@ -124,8 +126,8 @@ def tile_sinkhornattention_pa_t_kernel(tc, q_proj, k_proj, v, w_v, out):
                 nc.vector.tensor_copy(
                     out=v_words[:, 2 * h:2 * h + 2, :, :],
                     in_=pv[:].rearrange("q j u n -> q j n u"))
-            v_codes = wide.tile([P, 4 * P], U32, name="v_codes", tag="codes", align_bytes=64)
-            v_scales = wide.tile([P, 4 * P], U8, name="v_scales", tag="scales", align_bytes=64)
+            v_codes = coded.tile([P, 4 * P], U32, name="v_codes", tag="codes", align_bytes=64)
+            v_scales = coded.tile([P, 4 * P], U8, name="v_scales", tag="scales", align_bytes=64)
             nc.vector.quantize_mx(out=v_codes[:].bitcast(FP8X4), scales=v_scales[:], in_=v_grp[:])
             pvp = ps.tile([P, 4, D], F32, name="pvp", tag="ps")
             for j in range(4):
@@ -170,10 +172,14 @@ def tile_sinkhornattention_pa_t_kernel(tc, q_proj, k_proj, v, w_v, out):
                 st["s_first"] = small.tile([P, NT], F32, name="s_first")
             if i % 4 == 0:
                 st["half"].append(kern.tile([P, 4, T], F32, name="half", tag="half"))
-            for pair_ch in ((0, 1), (2, 3)):
+            wide_run = b != 2
+            for pair_ch in ((0, 1, 2, 3),) if wide_run else ((0, 1), (2, 3)):
                 banks = {}
                 for ch in pair_ch:
-                    pd = ps.tile([P, 512], F32, name="pd", tag="ps")
+                    if wide_run and i % 2 == 1:
+                        pd = ps_a.tile([P, 512], F32, name="pd", tag="acc")
+                    else:
+                        pd = ps.tile([P, 512], F32, name="pd", tag="ps")
                     nc.tensor.matmul(pd[:], lhsT=k_t[:, b, i, :], rhs=q_t[:, ch * 512:(ch + 1) * 512],
                                      start=True, stop=False)
                     banks[ch] = pd
@@ -191,15 +197,18 @@ def tile_sinkhornattention_pa_t_kernel(tc, q_proj, k_proj, v, w_v, out):
             nc.scalar.activation(out=rows(b, i), in_=rows(b, i), func=ACT.Sqrt, bias=k2[:, b, i:i + 1],
                                  scale=-2.0)
 
-        def shift_step(b):
+        def shift_bound(b):
             st = state[b]
             y_top = small.tile([P, NT], F32, name="y_top")
             nc.vector.tensor_reduce(out=y_top[:], in_=st["y_max"][:], axis=AX.X, op=ALU.max)
-            sq_min = small.tile([P, NT], F32, name="sq_min")
-            nc.vector.scalar_tensor_tensor(out=sq_min[:], in0=y_top[:], scalar=-2.0, in1=k2[:, b, :],
+            st["sq_min"] = small.tile([P, NT], F32, name="sq_min")
+            nc.vector.scalar_tensor_tensor(out=st["sq_min"][:], in0=y_top[:], scalar=-2.0, in1=k2[:, b, :],
                                            op0=ALU.mult, op1=ALU.add)
+
+        def shift_root(b):
+            st = state[b]
             st["shift"] = small.tile([P, NT], F32, name="shift")
-            nc.scalar.activation(out=st["shift"][:], in_=sq_min[:], func=ACT.Sqrt)
+            nc.scalar.activation(out=st["shift"][:], in_=st["sq_min"][:], func=ACT.Sqrt)
 
         def distances(b, before=None, stream=(), mine=()):
 
@@ -213,8 +222,9 @@ def tile_sinkhornattention_pa_t_kernel(tc, q_proj, k_proj, v, w_v, out):
                     plan_step(before, *mine[i // 2])
 
             for i in range(NT):
-                step(lambda i=i: (dots(b, i), beside(i)), lambda i=i: root(b, i))
-            step(None, None, lambda: shift_step(b))
+                step(lambda i=i: (dots(b, i), beside(i)),
+                     lambda i=i: (root(b, i), shift_root(b) if i == NT - 1 else None))
+            step(lambda: shift_bound(b))
             for block in mine[NT // 2:]:
                 step(lambda block=block: plan_step(before, *block))
 
@@ -242,24 +252,30 @@ def tile_sinkhornattention_pa_t_kernel(tc, q_proj, k_proj, v, w_v, out):
             nc.scalar.activation(out=rows(b, i), in_=rows(b, i), func=ACT.Copy,
                                  scale=state[b]["rho"][:, i:i + 1])
 
-        def column_sums(b, i):
+        def column_sums(b, i, v_banks):
             st = state[b]
             if i == 0:
                 for g in range(4):
-                    st["acc", g] = ps_a.tile([P, 4, P], F32, name="acc", tag="acc")
+                    if b % 2 == 0:
+                        st["acc", g] = ps_a.tile([P, 4, P], F32, name="acc", tag="acc")
+                    else:
+                        st["acc", g] = ps.tile([P, 4, P], F32, name="acc", tag="ps")
             for a in range(TT):
                 nc.tensor.matmul(st["acc", a // 4][:, a % 4, :], lhsT=rows(b, i)[:, a * P:(a + 1) * P], rhs=ident_f[:],
                                  is_transpose=True,
                                  start=(i == 0 and a % 4 == 0), stop=(i == NT - 1 and a % 4 == 3))
             if i == NT - 1:
                 st["r_sum"] = small.tile([P, TT], F32, name="r_sum")
-                for g in range(V_BANKS):
-                    nc.vector.tensor_reduce(out=st["r_sum"][:, 4 * g:4 * g + 4],
-                                            in_=st["acc", g][:], axis=AX.X, op=ALU.add)
-                for a in range(4 * V_BANKS, TT):
+                for a in range(4 * v_banks, TT):
                     drop = small.tile([P, D], F32, name="drop")
                     nc.scalar.activation(out=drop[:], in_=st["acc", a // 4][:, a % 4, :], func=ACT.Copy,
                                          accum_out=st["r_sum"][:, a:a + 1])
+
+        def reduce_sums(b, v_banks):
+            st = state[b]
+            for g in range(v_banks):
+                nc.vector.tensor_reduce(out=st["r_sum"][:, 4 * g:4 * g + 4],
+                                        in_=st["acc", g][:], axis=AX.X, op=ALU.add)
 
         def spread(b):
             st = state[b]
@@ -278,15 +294,26 @@ def tile_sinkhornattention_pa_t_kernel(tc, q_proj, k_proj, v, w_v, out):
             if it > 0:
                 state[b]["s_n"] = small.tile([P, NT], F32, name="s_n")
             for i in range(NT):
-                last = (lambda: spread(b)) if i == NT - 1 else None
+                end = i == NT - 1
                 if it == 0:
-                    step(lambda i=i: exponent(b, i), lambda i=i: invert(b, i, "s_first"),
-                         lambda i=i: scale_first(b, i), lambda i=i: column_sums(b, i), last)
+                    parts = [lambda i=i: exponent(b, i), lambda i=i: invert(b, i, "s_first"),
+                             lambda i=i: scale_first(b, i)]
+                    sums, reduces, spreads, v_banks = 3, 3, 4, 4
                 else:
-                    hurry = it == ITERS - 1 and b % 2 == 1 and i == NT - 1
-                    step(lambda i=i: row_sum(b, i), lambda i=i: invert_scale(b, i), None,
-                         lambda i=i, hurry=hurry: (column_sums(b, i), spread(b) if hurry else None),
-                         None if hurry else last)
+                    parts = [lambda i=i: row_sum(b, i), lambda i=i: invert_scale(b, i)]
+                    sums, reduces, spreads, v_banks = 2, 3, 4, 2
+                    if it == ITERS - 1 and b % 2 == 1:
+                        sums, reduces, spreads = 2, 3, 3
+                later_parts = {}
+                later_parts.setdefault(sums, []).append(lambda i=i: column_sums(b, i, v_banks))
+                if end:
+                    later_parts.setdefault(reduces, []).append(lambda: reduce_sums(b, v_banks))
+                    later_parts.setdefault(spreads, []).append(lambda: spread(b))
+                while len(parts) <= max(later_parts):
+                    parts.append(None)
+                for delay, calls in later_parts.items():
+                    parts[delay] = lambda first=parts[delay], calls=calls: [call() for call in [first] + calls if call]
+                step(*parts)
 
         def plan(b, g, c):
             st = state[b]
@@ -302,8 +329,8 @@ def tile_sinkhornattention_pa_t_kernel(tc, q_proj, k_proj, v, w_v, out):
         def quantise(b, g, c):
             st = state[b]
             if ("codes", g) not in st:
-                st["codes", g] = wide.tile([P, 2, 512], U32, name="codes", tag="codes", align_bytes=64)
-                st["scales", g] = wide.tile([P, 2, 512], U8, name="scales", tag="scales", align_bytes=64)
+                st["codes", g] = coded.tile([P, 2, 512], U32, name="codes", tag="codes", align_bytes=64)
+                st["scales", g] = coded.tile([P, 2, 512], U8, name="scales", tag="scales", align_bytes=64)
             nc.vector.quantize_mx(out=st["codes", g][:, c, :].bitcast(FP8X4), scales=st["scales", g][:, c, :],
                                   in_=st["grp", g, c][:].rearrange("p t j -> p (t j)"))
 
@@ -333,32 +360,32 @@ def tile_sinkhornattention_pa_t_kernel(tc, q_proj, k_proj, v, w_v, out):
             plan(b, g, c)
             later(lambda: code(b, g, c))
 
-        def turn(b, g, a):
+        def turn(b, g, c, a):
             st = state[b]
             if a == 0:
-                st["grp", g, 1] = group.tile([P, 512, 4], BF16, name="grp", tag="g4", align_bytes=64)
+                st["grp", g, c] = group.tile([P, 512, 4], BF16, name="grp", tag="g4", align_bytes=64)
             st["turned"] = ps_a.tile([P, 4, P], F32, name="turned", tag="acc")
             cols = slice(g * 512 + a * P, g * 512 + (a + 1) * P)
             for j in range(4):
-                nc.tensor.transpose(st["turned"][:, j, :], st["half"][1][:, j, cols], ident_f[:])
+                nc.tensor.transpose(st["turned"][:, j, :], st["half"][c][:, j, cols], ident_f[:])
 
-        def weigh(b, g, a):
+        def weigh(b, g, c, a):
             st = state[b]
             st["mid", a] = mids.tile([P, 4, P], F32, name="mid")
             nc.scalar.activation(out=st["mid", a][:], in_=st["turned"][:], func=ACT.Copy,
                                  scale=w_cols[:, b, 4 * g + a:4 * g + a + 1])
 
-        def turn_back(b, g, a):
+        def turn_back(b, g, c, a):
             st = state[b]
             back = ps_a.tile([P, 4, P], F32, name="back", tag="acc")
             for j in range(4):
                 nc.tensor.transpose(back[:, j, :], st["mid", a][:, j, :], ident_f[:])
-            nc.scalar.copy(out=st["grp", g, 1][:, a * P:(a + 1) * P, :], in_=back[:].rearrange("p j t -> p t j"))
+            nc.scalar.copy(out=st["grp", g, c][:, a * P:(a + 1) * P, :], in_=back[:].rearrange("p j t -> p t j"))
             if a == 3:
-                later(lambda: code(b, g, 1))
+                later(lambda: code(b, g, c))
 
         def ticks(b, s_blocks):
-            units = [(g, a) for g in range(s_blocks) for a in range(4)]
+            units = [(g, c, a) for g, c in ORDER[:s_blocks] for a in range(4)]
 
             def tick(u):
                 if 0 <= u - 1 < len(units):
@@ -370,7 +397,7 @@ def tile_sinkhornattention_pa_t_kernel(tc, q_proj, k_proj, v, w_v, out):
             return [lambda u=u: tick(u) for u in range(len(units) + 2)]
 
         def blocks(s_blocks):
-            return [(g, 0) for g in range(4)] + [(g, 1) for g in range(s_blocks, 4)]
+            return sorted(ORDER[s_blocks:])
 
         def attend(b, stream=(), first_tick=0):
             stream = list(stream)

@@ -19,6 +19,7 @@ NT = N // P
 TT = T // P
 V_BANKS = 3
 ORDER = ((0, 1), (1, 1), (2, 1), (3, 1), (3, 0), (2, 0), (1, 0), (0, 0))
+AHEAD = 0
 FIRST_TICK = 3
 MID_BLOCKS, TAIL_BLOCKS = 3, 4
 FLOPS = 2 * B * (2 * T * N * D + N * VD * D)
@@ -35,6 +36,8 @@ def tile_sinkhornattention_pa_t_kernel(tc, q_proj, k_proj, v, w_v, out):
         small = ctx.enter_context(tc.tile_pool(name="small", bufs=4))
         wide = ctx.enter_context(tc.tile_pool(name="wide", bufs=2))
         one = ctx.enter_context(tc.tile_pool(name="one", bufs=1))
+        keys = ctx.enter_context(tc.tile_pool(name="keys", bufs=2))
+        vals = ctx.enter_context(tc.tile_pool(name="vals", bufs=2))
         coded = ctx.enter_context(tc.tile_pool(name="coded", bufs=3))
         scrap = ctx.enter_context(tc.tile_pool(name="scrap", bufs=3))
         ps_a = ctx.enter_context(tc.psum_pool(name="ps_a", bufs=4))
@@ -79,11 +82,15 @@ def tile_sinkhornattention_pa_t_kernel(tc, q_proj, k_proj, v, w_v, out):
         q_sb = group.tile([P, TT, D], BF16, name="q_sb", tag="g4", align_bytes=64)
         for g in range(0, TT, 8):
             nc.sync.dma_start(out=q_sb[:, g:g + 8, :], in_=q_proj.rearrange("(p a) d -> p a d", a=TT)[:, g:g + 8, :])
-        k_all = const.tile([P, B, NT, D], BF16, name="k_all")
-        for b in range(B):
+
+        def k_load(b):
+            state[b]["k_sb"] = keys.tile([P, NT, D], BF16, name="k_sb")
             nc.sync.dma_start(
-                out=k_all[:, b, :, :].rearrange("p (c j) d -> p c j d", c=2),
+                out=state[b]["k_sb"][:].rearrange("p (c j) d -> p c j d", c=2),
                 in_=k_proj[b].rearrange("(c p j) d -> p c j d", c=2, j=4))
+
+        k_load(0)
+        k_load(1)
         for g in range(4):
             pt = ps.tile([P, 512], BF16, name="pt", tag="ps")
             for a in range(4):
@@ -96,7 +103,7 @@ def tile_sinkhornattention_pa_t_kernel(tc, q_proj, k_proj, v, w_v, out):
             if a % 4 == 3:
                 nc.scalar.activation(out=nq2h[:, a - 3:a + 1], in_=q2[:, a - 3:a + 1], func=ACT.Copy, scale=-0.5)
         k_sq = wide.tile([P, NT, D], F32, name="k_sq", tag="w8")
-        nc.vector.tensor_tensor(out=k_sq[:], in0=k_all[:, 0, :, :], in1=k_all[:, 0, :, :], op=ALU.mult)
+        nc.vector.tensor_tensor(out=k_sq[:], in0=state[0]["k_sb"][:], in1=state[0]["k_sb"][:], op=ALU.mult)
         nc.vector.tensor_reduce(out=k2[:, 0, :], in_=k_sq[:], axis=AX.X, op=ALU.add)
         nc.vector.tensor_scalar(out=k2h[:, 0, :], in0=k2[:, 0, :], scalar1=0.5, scalar2=None, op0=ALU.mult)
 
@@ -109,51 +116,73 @@ def tile_sinkhornattention_pa_t_kernel(tc, q_proj, k_proj, v, w_v, out):
                 out=wv_codes[:].bitcast(FP8X4), scales=wv_scales[:],
                 in_=wv_grp[:].rearrange("q c t -> q (c t)"))
 
-        def vp_step(b, c):
-            if c == 0:
-                v_new = wide.tile([P, 2, 4, VD], BF16, name="v_sb", tag="w8")
-                nc.sync.dma_start(out=v_new[:], in_=v[b].rearrange("(c p j) f -> p c j f", c=2, j=4))
-                state[b]["v_sb"] = v_new
-            v_sb = state[b]["v_sb"]
-            v_grp = group.tile([P, 4 * P * 4], BF16, name="v_grp", tag="g4", align_bytes=64)
-            v_words = v_grp[:].bitcast(F32).rearrange("q (j n u) -> q j n u", j=4, u=2)
+        def v_load(b):
+            for c in range(2):
+                v_sb = vals.tile([P, 4, VD], BF16, name="v_sb")
+                nc.sync.dma_start(
+                    out=v_sb[:], in_=v[b, c * 4 * P:(c + 1) * 4 * P, :].rearrange("(p j) f -> p j f", j=4))
+                state[b]["v_sb", c] = v_sb
+
+        def v_turn(b, c):
+            st = state[b]
             for h in range(2):
-                pv = ps.tile([P, 2, 2, P], F32, name="pv", tag="ps")
+                st["pv", h] = ps.tile([P, 2, 2, P], F32, name="pv", tag="ps")
                 for jj in range(2):
-                    words = v_sb[:, c, 2 * h + jj, :].bitcast(F32)
+                    words = st["v_sb", c][:, 2 * h + jj, :].bitcast(F32)
                     for u in range(2):
-                        nc.tensor.transpose(pv[:, jj, u, :], words[:, u * P:(u + 1) * P], ident_f[:])
+                        nc.tensor.transpose(st["pv", h][:, jj, u, :], words[:, u * P:(u + 1) * P], ident_f[:])
+
+        def v_group(b):
+            st = state[b]
+            st["v_grp"] = group.tile([P, 4 * P * 4], BF16, name="v_grp", tag="g4", align_bytes=64)
+            v_words = st["v_grp"][:].bitcast(F32).rearrange("q (j n u) -> q j n u", j=4, u=2)
+            for h in range(2):
                 nc.vector.tensor_copy(
                     out=v_words[:, 2 * h:2 * h + 2, :, :],
-                    in_=pv[:].rearrange("q j u n -> q j n u"))
-            v_codes = coded.tile([P, 4 * P], U32, name="v_codes", tag="codes", align_bytes=64)
-            v_scales = coded.tile([P, 4 * P], U8, name="v_scales", tag="scales", align_bytes=64)
-            nc.vector.quantize_mx(out=v_codes[:].bitcast(FP8X4), scales=v_scales[:], in_=v_grp[:])
-            pvp = ps.tile([P, 4, D], F32, name="pvp", tag="ps")
+                    in_=st["pv", h][:].rearrange("q j u n -> q j n u"))
+
+        def v_quantise(b):
+            st = state[b]
+            st["v_codes"] = coded.tile([P, 4 * P], U32, name="v_codes", tag="codes", align_bytes=64)
+            st["v_scales"] = coded.tile([P, 4 * P], U8, name="v_scales", tag="scales", align_bytes=64)
+            nc.vector.quantize_mx(out=st["v_codes"][:].bitcast(FP8X4), scales=st["v_scales"][:],
+                                  in_=st["v_grp"][:])
+
+        def v_multiply(b):
+            st = state[b]
+            st["pvp"] = ps.tile([P, 4, D], F32, name="pvp", tag="ps")
             for j in range(4):
                 nc.tensor.matmul_mx(
-                    out=pvp[:, j, :],
-                    lhsT=v_codes[:, j * P:(j + 1) * P].bitcast(FP8X4),
-                    lhsT_scale=v_scales[:, j * P:(j + 1) * P],
+                    out=st["pvp"][:, j, :],
+                    lhsT=st["v_codes"][:, j * P:(j + 1) * P].bitcast(FP8X4),
+                    lhsT_scale=st["v_scales"][:, j * P:(j + 1) * P],
                     rhs=wv_codes[:].bitcast(FP8X4), rhs_scale=wv_scales[:],
                     start=True, stop=True)
-            vp_grp = one.tile([P, D, 4], BF16, name="vp_grp", align_bytes=64)
-            nc.vector.tensor_copy(out=vp_grp[:], in_=pvp[:].rearrange("p j d -> p d j"))
+
+        def vp_group(b):
+            st = state[b]
+            st["vp_grp"] = one.tile([P, D, 4], BF16, name="vp_grp", align_bytes=64)
+            nc.vector.tensor_copy(out=st["vp_grp"][:], in_=st["pvp"][:].rearrange("p j d -> p d j"))
+
+        def vp_quantise(b, c):
             nc.vector.quantize_mx(
                 out=vp_codes[:, b, c, :].bitcast(FP8X4), scales=vp_scales[:, b, c, :],
-                in_=vp_grp[:].rearrange("p d j -> p (d j)"))
+                in_=state[b]["vp_grp"][:].rearrange("p d j -> p (d j)"))
 
-        def value_projection(pair):
-            if pair[0] == 0:
-                step(wv_step)
-            for b in pair:
-                for c in range(2):
-                    step(lambda b=b, c=c: vp_step(b, c))
+        def value_projection(b):
+            parts = []
+            for c in range(2):
+                parts += [lambda c=c: v_turn(b, c), lambda: v_group(b), lambda: (v_quantise(b), v_multiply(b)),
+                          lambda c=c: (vp_group(b), vp_quantise(b, c))]
+            if b % 2 == 0:
+                last_quantise = parts[6]
+                parts[6] = lambda: (last_quantise(), v_load(b + 1))
+            return parts
 
         def square_keys(b):
             for i in range(NT):
                 drop = small.tile([P, D], F32, name="drop")
-                nc.scalar.activation(out=drop[:], in_=k_all[:, b, i, :], func=ACT.Square,
+                nc.scalar.activation(out=drop[:], in_=state[b]["k_sb"][:, i, :], func=ACT.Square,
                                      accum_out=k2[:, b, i:i + 1])
             nc.scalar.activation(out=k2h[:, b, :], in_=k2[:, b, :], func=ACT.Copy, scale=0.5)
 
@@ -161,8 +190,11 @@ def tile_sinkhornattention_pa_t_kernel(tc, q_proj, k_proj, v, w_v, out):
             for g in range(2):
                 pk = ps.tile([P, 4, P], BF16, name="pk", tag="ps")
                 for a in range(4):
-                    nc.tensor.transpose(pk[:, a, :], k_all[:, b, 4 * g + a, :], ident_b[:])
-                nc.vector.tensor_copy(out=k_t[:, b, 4 * g:4 * g + 4, :], in_=pk[:])
+                    nc.tensor.transpose(pk[:, a, :], state[b]["k_sb"][:, 4 * g + a, :], ident_b[:])
+                if b == 0:
+                    nc.vector.tensor_copy(out=k_t[:, b, 4 * g:4 * g + 4, :], in_=pk[:])
+                else:
+                    nc.scalar.copy(out=k_t[:, b, 4 * g:4 * g + 4, :], in_=pk[:])
 
         def dots(b, i):
             st = state[b]
@@ -216,6 +248,8 @@ def tile_sinkhornattention_pa_t_kernel(tc, q_proj, k_proj, v, w_v, out):
                 if i == 3 and b + 1 < B:
                     square_keys(b + 1)
                     turn_keys(b + 1)
+                    if b + 2 < B:
+                        k_load(b + 2)
                 for tick in stream[2 * i:2 * i + 2]:
                     tick()
                 if i % 2 == 1 and i // 2 < len(mine):
@@ -233,30 +267,30 @@ def tile_sinkhornattention_pa_t_kernel(tc, q_proj, k_proj, v, w_v, out):
             nc.scalar.activation(out=rows(b, i), in_=rows(b, i), func=ACT.Exp, bias=st["shift"][:, i:i + 1],
                                  scale=-1.0, accum_out=st["s_first"][:, i:i + 1])
 
-        def row_sum(b, i):
+        def row_sum(b, it, i):
             st = state[b]
             junk = scrap.tile([P, T], BF16, name="junk")
             nc.vector.scalar_tensor_tensor(
                 out=junk[:], in0=rows(b, i), scalar=float(N), in1=st["w_all"][:],
-                op0=ALU.mult, op1=ALU.mult, accum_out=st["s_n"][:, i:i + 1])
+                op0=ALU.mult, op1=ALU.mult, accum_out=st["s_n", it][:, i:i + 1])
 
-        def invert(b, i, sums):
-            nc.vector.reciprocal(out=state[b]["rho"][:, i:i + 1], in_=state[b][sums][:, i:i + 1])
+        def invert_first(b, i):
+            nc.vector.reciprocal(out=state[b]["rho", 0][:, i:i + 1], in_=state[b]["s_first"][:, i:i + 1])
 
         def scale_first(b, i):
-            nc.vector.tensor_scalar(out=rows(b, i), in0=rows(b, i), scalar1=state[b]["rho"][:, i:i + 1],
+            nc.vector.tensor_scalar(out=rows(b, i), in0=rows(b, i), scalar1=state[b]["rho", 0][:, i:i + 1],
                                     scalar2=1.0 / N, op0=ALU.mult, op1=ALU.mult)
 
-        def invert_scale(b, i):
-            invert(b, i, "s_n")
-            nc.scalar.activation(out=rows(b, i), in_=rows(b, i), func=ACT.Copy,
-                                 scale=state[b]["rho"][:, i:i + 1])
+        def invert_scale(b, it, i):
+            rho = state[b]["rho", it]
+            nc.vector.reciprocal(out=rho[:, i:i + 1], in_=state[b]["s_n", it][:, i:i + 1])
+            nc.scalar.activation(out=rows(b, i), in_=rows(b, i), func=ACT.Copy, scale=rho[:, i:i + 1])
 
-        def column_sums(b, i, v_banks):
+        def column_sums(b, i, v_banks, first_round):
             st = state[b]
             if i == 0:
                 for g in range(4):
-                    if b % 2 == 0:
+                    if b % 2 == 0 or first_round:
                         st["acc", g] = ps_a.tile([P, 4, P], F32, name="acc", tag="acc")
                     else:
                         st["acc", g] = ps.tile([P, 4, P], F32, name="acc", tag="ps")
@@ -277,43 +311,69 @@ def tile_sinkhornattention_pa_t_kernel(tc, q_proj, k_proj, v, w_v, out):
                 nc.vector.tensor_reduce(out=st["r_sum"][:, 4 * g:4 * g + 4],
                                         in_=st["acc", g][:], axis=AX.X, op=ALU.add)
 
-        def spread(b):
+        def spread(b, it):
             st = state[b]
             nc.vector.reciprocal(out=w_cols[:, b, 0:TT], in_=st["r_sum"][:])
             w_turn = small.tile([P, 32], F32, name="w_turn", align_bytes=64)
             nc.vector.transpose(out=w_turn[:], in_=w_cols[:, b, :])
-            corner = out[b, st["round"] * TT:(st["round"] + 1) * TT, :]
+            corner = out[b, it * TT:(it + 1) * TT, :]
             for quad in range(0, P, 32):
                 nc.sync.dma_start(out=corner[:, quad:quad + 32], in_=w_turn[quad:quad + TT, :])
             st["w_all"] = wide.tile([P, T], F32, name="w_all", tag="w8")
             nc.sync.dma_start(out=st["w_all"][:], in_=corner.rearrange("a p -> (a p)").partition_broadcast(P))
 
-        def sinkhorn_round(b, it):
-            state[b]["rho"] = small.tile([P, NT], F32, name="rho")
-            state[b]["round"] = it
-            if it > 0:
-                state[b]["s_n"] = small.tile([P, NT], F32, name="s_n")
+        def round_steps(b, it):
+            st = state[b]
+            st["rho", it] = small.tile([P, NT], F32, name="rho")
+            if it == 0:
+                projection = value_projection(b)
+            else:
+                st["s_n", it] = small.tile([P, NT], F32, name="s_n")
+            steps = []
             for i in range(NT):
-                end = i == NT - 1
                 if it == 0:
-                    parts = [lambda i=i: exponent(b, i), lambda i=i: invert(b, i, "s_first"),
+                    parts = [lambda i=i: exponent(b, i), lambda i=i: invert_first(b, i),
                              lambda i=i: scale_first(b, i)]
+                    while len(parts) < 1:
+                        parts.append(None)
+                    parts[0] = lambda first=parts[0], i=i: [call() for call in (first, projection[i]) if call]
                     sums, reduces, spreads, v_banks = 3, 3, 4, 4
                 else:
-                    parts = [lambda i=i: row_sum(b, i), lambda i=i: invert_scale(b, i)]
-                    sums, reduces, spreads, v_banks = 2, 3, 4, 2
+                    parts = [lambda i=i: row_sum(b, it, i), lambda i=i: invert_scale(b, it, i)]
+                    sums, reduces, spreads, v_banks = 3, 3, 5, 2
                     if it == ITERS - 1 and b % 2 == 1:
-                        sums, reduces, spreads = 2, 3, 3
-                later_parts = {}
-                later_parts.setdefault(sums, []).append(lambda i=i: column_sums(b, i, v_banks))
-                if end:
-                    later_parts.setdefault(reduces, []).append(lambda: reduce_sums(b, v_banks))
-                    later_parts.setdefault(spreads, []).append(lambda: spread(b))
-                while len(parts) <= max(later_parts):
-                    parts.append(None)
-                for delay, calls in later_parts.items():
-                    parts[delay] = lambda first=parts[delay], calls=calls: [call() for call in [first] + calls if call]
+                        sums, reduces, spreads = 3, 3, 3
+                extra = {}
+                extra.setdefault(sums, []).append(lambda i=i: column_sums(b, i, v_banks, it == 0))
+                if i == NT - 1:
+                    extra.setdefault(reduces, []).append(lambda: reduce_sums(b, v_banks))
+                    extra.setdefault(spreads, []).append(lambda: spread(b, it))
+                steps.append(merged(parts, [extra.get(d) and (lambda calls=extra[d]: [call() for call in calls])
+                                            for d in range(max(extra) + 1)]))
+            return steps
+
+        def merged(parts, others):
+            both = []
+            for d in range(max(len(parts), len(others))):
+                calls = [side[d] for side in (parts, others) if d < len(side) and side[d]]
+                both.append((lambda calls=calls: [call() for call in calls]) if calls else None)
+            return both
+
+        def rounds(pair):
+            first_steps = round_steps(pair[0], 0)
+            second_steps = round_steps(pair[1], 0)
+            for parts in first_steps + second_steps[:NT - AHEAD]:
                 step(*parts)
+            ahead = round_steps(pair[0], 1)
+            for k in range(AHEAD):
+                step(*merged(second_steps[NT - AHEAD + k], ahead[k]))
+            for parts in ahead[AHEAD:]:
+                step(*parts)
+            for it in range(1, ITERS):
+                for b in pair:
+                    if (b, it) != (pair[0], 1):
+                        for parts in round_steps(b, it):
+                            step(*parts)
 
         def plan(b, g, c):
             st = state[b]
@@ -416,10 +476,10 @@ def tile_sinkhornattention_pa_t_kernel(tc, q_proj, k_proj, v, w_v, out):
                     distances(b, b - 1, rest, blocks(MID_BLOCKS))
                 else:
                     distances(b)
-            value_projection(pair)
-            for it in range(ITERS):
-                for b in pair:
-                    sinkhorn_round(b, it)
+            if first == 0:
+                step(wv_step)
+            step(lambda b=first: v_load(b))
+            rounds(pair)
         rest = attend(B - 2, ticks(B - 1, TAIL_BLOCKS), FIRST_TICK)
         for block in blocks(TAIL_BLOCKS):
             step(lambda block=block, mine=rest[:2]: (plan_step(B - 1, *block), [tick() for tick in mine]))

@@ -19,7 +19,6 @@ NT = N // P
 TT = T // P
 V_BANKS = 3
 ORDER = ((0, 1), (1, 1), (2, 1), (3, 1), (3, 0), (2, 0), (1, 0), (0, 0))
-AHEAD = 0
 FIRST_TICK = 3
 MID_BLOCKS, TAIL_BLOCKS = 3, 4
 FLOPS = 2 * B * (2 * T * N * D + N * VD * D)
@@ -32,7 +31,7 @@ def tile_sinkhornattention_pa_t_kernel(tc, q_proj, k_proj, v, w_v, out):
         const = ctx.enter_context(tc.tile_pool(name="const", bufs=1))
         kern = ctx.enter_context(tc.tile_pool(name="kern", bufs=4))
         group = ctx.enter_context(tc.tile_pool(name="group", bufs=4))
-        mids = ctx.enter_context(tc.tile_pool(name="mids", bufs=3))
+        mids = ctx.enter_context(tc.tile_pool(name="mids", bufs=4))
         small = ctx.enter_context(tc.tile_pool(name="small", bufs=4))
         wide = ctx.enter_context(tc.tile_pool(name="wide", bufs=2))
         one = ctx.enter_context(tc.tile_pool(name="one", bufs=1))
@@ -50,12 +49,14 @@ def tile_sinkhornattention_pa_t_kernel(tc, q_proj, k_proj, v, w_v, out):
         q_t = const.tile([P, T], BF16, name="q_t")
         nq2h = const.tile([P, TT], F32, name="nq2h")
         w_cols = const.tile([P, B, 32], F32, name="w_cols", align_bytes=64)
+        rho_all = const.tile([P, B, 2, NT], F32, name="rho_all")
+        s_all = const.tile([P, B, 2, NT], F32, name="s_all")
         nc.gpsimd.memset(w_cols[:], 1.0)
         k_t = const.tile([P, B, NT, P], BF16, name="k_t")
         k2 = const.tile([P, B, NT], F32, name="k2")
         k2h = const.tile([P, B, NT], F32, name="k2h")
-        vp_codes = const.tile([P, B, 2, P], U32, name="vp_codes", align_bytes=64)
-        vp_scales = const.tile([P, B, 2, P], U8, name="vp_scales", align_bytes=64)
+        vp_codes = const.tile([P, 2, 2, P], U32, name="vp_codes", align_bytes=64)
+        vp_scales = const.tile([P, 2, 2, P], U8, name="vp_scales", align_bytes=64)
         wv_codes = const.tile([P, D], U32, name="wv_codes", align_bytes=64)
         wv_scales = const.tile([P, D], U8, name="wv_scales", align_bytes=64)
 
@@ -116,12 +117,11 @@ def tile_sinkhornattention_pa_t_kernel(tc, q_proj, k_proj, v, w_v, out):
                 out=wv_codes[:].bitcast(FP8X4), scales=wv_scales[:],
                 in_=wv_grp[:].rearrange("q c t -> q (c t)"))
 
-        def v_load(b):
-            for c in range(2):
-                v_sb = vals.tile([P, 4, VD], BF16, name="v_sb")
-                nc.sync.dma_start(
-                    out=v_sb[:], in_=v[b, c * 4 * P:(c + 1) * 4 * P, :].rearrange("(p j) f -> p j f", j=4))
-                state[b]["v_sb", c] = v_sb
+        def v_load(b, c):
+            v_sb = vals.tile([P, 4, VD], BF16, name="v_sb")
+            nc.sync.dma_start(
+                out=v_sb[:], in_=v[b, c * 4 * P:(c + 1) * 4 * P, :].rearrange("(p j) f -> p j f", j=4))
+            state[b]["v_sb", c] = v_sb
 
         def v_turn(b, c):
             st = state[b]
@@ -166,18 +166,31 @@ def tile_sinkhornattention_pa_t_kernel(tc, q_proj, k_proj, v, w_v, out):
 
         def vp_quantise(b, c):
             nc.vector.quantize_mx(
-                out=vp_codes[:, b, c, :].bitcast(FP8X4), scales=vp_scales[:, b, c, :],
+                out=vp_codes[:, b % 2, c, :].bitcast(FP8X4), scales=vp_scales[:, b % 2, c, :],
                 in_=state[b]["vp_grp"][:].rearrange("p d j -> p (d j)"))
 
-        def value_projection(b):
-            parts = []
-            for c in range(2):
-                parts += [lambda c=c: v_turn(b, c), lambda: v_group(b), lambda: (v_quantise(b), v_multiply(b)),
-                          lambda c=c: (vp_group(b), vp_quantise(b, c))]
-            if b % 2 == 0:
-                last_quantise = parts[6]
-                parts[6] = lambda: (last_quantise(), v_load(b + 1))
-            return parts
+        def value_projection(first):
+            halves = [(b, c) for b in (first, first + 1) for c in range(2)]
+
+            def part(h, s):
+                b, c = halves[h]
+                if s == 0:
+                    v_turn(b, c)
+                elif s == 1:
+                    v_group(b)
+                    if h + 2 < len(halves):
+                        v_load(*halves[h + 2])
+                elif s == 2:
+                    v_quantise(b)
+                    v_multiply(b)
+                else:
+                    vp_group(b)
+                    vp_quantise(b, c)
+            beside = [[] for n in range(2 * NT)]
+            for h in range(len(halves)):
+                for s in range(4):
+                    beside[2 * h + s + 0].insert(0, lambda h=h, s=s: part(h, s))
+            return beside
 
         def square_keys(b):
             for i in range(NT):
@@ -281,29 +294,72 @@ def tile_sinkhornattention_pa_t_kernel(tc, q_proj, k_proj, v, w_v, out):
             nc.vector.tensor_scalar(out=rows(b, i), in0=rows(b, i), scalar1=state[b]["rho", 0][:, i:i + 1],
                                     scalar2=1.0 / N, op0=ALU.mult, op1=ALU.mult)
 
-        def invert_scale(b, it, i):
-            rho = state[b]["rho", it]
-            nc.vector.reciprocal(out=rho[:, i:i + 1], in_=state[b]["s_n", it][:, i:i + 1])
-            nc.scalar.activation(out=rows(b, i), in_=rows(b, i), func=ACT.Copy, scale=rho[:, i:i + 1])
+        def invert_row(b, it, i):
+            nc.vector.reciprocal(out=state[b]["rho", it][:, i:i + 1], in_=state[b]["s_n", it][:, i:i + 1])
 
-        def column_sums(b, i, v_banks, first_round):
+        def scalar_scale(b, it, i):
+            nc.scalar.activation(out=rows(b, i), in_=rows(b, i), func=ACT.Copy,
+                                 scale=state[b]["rho", it][:, i:i + 1])
+
+        def vector_scale(b, it, i):
+            nc.vector.tensor_scalar(out=rows(b, i), in0=rows(b, i), scalar1=state[b]["rho", it][:, i:i + 1],
+                                    scalar2=None, op0=ALU.mult)
+
+        def turn_tiles(b, u):
             st = state[b]
-            if i == 0:
+            st["turned", u % 4] = ps.tile([P, 2, 2, P], F32, name="turned", tag="ps")
+            for h in range(2):
+                for t in range(2):
+                    a = 2 * u + h
+                    nc.tensor.transpose(st["turned", u % 4][:, h, t, :], rows(b, NT - 2 + t)[:, a * P:(a + 1) * P],
+                                        ident_f[:])
+
+        def weigh_tiles(b, u):
+            st = state[b]
+            st["mid", u % 4] = mids.tile([P, 2, 2, P], F32, name="mid")
+            for h in range(2):
+                a = 2 * u + h
+                nc.scalar.activation(out=st["mid", u % 4][:, h, :, :], in_=st["turned", u % 4][:, h, :, :],
+                                     func=ACT.Copy, scale=w_cols[:, b, a:a + 1])
+
+        def add_tiles(b, u):
+            st = state[b]
+            if u == 0:
+                st["racc"] = ps.tile([P, 2, P], F32, name="racc", tag="ps")
+            for h in range(2):
+                for t in range(2):
+                    nc.tensor.matmul(st["racc"][:, t, :], lhsT=st["mid", u % 4][:, h, t, :], rhs=ident_f[:],
+                                     is_transpose=True, start=(u == 0 and h == 0 and t == 0),
+                                     stop=(u == 7 and h == 1 and t == 1))
+
+        def reduce_turned(b, it):
+            for t in range(2):
+                drop = small.tile([P, D], F32, name="drop")
+                nc.vector.tensor_scalar(out=drop[:], in0=state[b]["racc"][:, t, :], scalar1=float(N), scalar2=None,
+                                        op0=ALU.mult, op1=ALU.add,
+                                        accum_out=state[b]["s_n", it][:, NT - 2 + t:NT - 1 + t])
+
+        def invert_turned(b, it):
+            nc.vector.reciprocal(out=state[b]["rho", it][:, NT - 2:NT], in_=state[b]["s_n", it][:, NT - 2:NT])
+
+
+        def column_sums(b, i, first, last):
+            st = state[b]
+            if first:
                 for g in range(4):
-                    if b % 2 == 0 or first_round:
-                        st["acc", g] = ps_a.tile([P, 4, P], F32, name="acc", tag="acc")
-                    else:
-                        st["acc", g] = ps.tile([P, 4, P], F32, name="acc", tag="ps")
+                    st["acc", g] = ps_a.tile([P, 4, P], F32, name="acc", tag="acc")
             for a in range(TT):
                 nc.tensor.matmul(st["acc", a // 4][:, a % 4, :], lhsT=rows(b, i)[:, a * P:(a + 1) * P], rhs=ident_f[:],
                                  is_transpose=True,
-                                 start=(i == 0 and a % 4 == 0), stop=(i == NT - 1 and a % 4 == 3))
-            if i == NT - 1:
-                st["r_sum"] = small.tile([P, TT], F32, name="r_sum")
-                for a in range(4 * v_banks, TT):
-                    drop = small.tile([P, D], F32, name="drop")
-                    nc.scalar.activation(out=drop[:], in_=st["acc", a // 4][:, a % 4, :], func=ACT.Copy,
-                                         accum_out=st["r_sum"][:, a:a + 1])
+                                 start=(first and a % 4 == 0), stop=(last and a % 4 == 3))
+
+        def scalar_sums(b, v_banks):
+            st = state[b]
+            st["r_sum"] = small.tile([P, TT], F32, name="r_sum")
+            for a in range(4 * v_banks, TT):
+                drop = small.tile([P, D], F32, name="drop")
+                nc.scalar.activation(out=drop[:], in_=st["acc", a // 4][:, a % 4, :], func=ACT.Copy,
+                                     accum_out=st["r_sum"][:, a:a + 1])
 
         def reduce_sums(b, v_banks):
             st = state[b]
@@ -311,9 +367,13 @@ def tile_sinkhornattention_pa_t_kernel(tc, q_proj, k_proj, v, w_v, out):
                 nc.vector.tensor_reduce(out=st["r_sum"][:, 4 * g:4 * g + 4],
                                         in_=st["acc", g][:], axis=AX.X, op=ALU.add)
 
-        def spread(b, it):
+        def spread_invert(b):
+            nc.vector.reciprocal(out=w_cols[:, b, 0:TT], in_=state[b]["r_sum"][:])
+
+        def spread(b, it, inverted=False):
             st = state[b]
-            nc.vector.reciprocal(out=w_cols[:, b, 0:TT], in_=st["r_sum"][:])
+            if not inverted:
+                spread_invert(b)
             w_turn = small.tile([P, 32], F32, name="w_turn", align_bytes=64)
             nc.vector.transpose(out=w_turn[:], in_=w_cols[:, b, :])
             corner = out[b, it * TT:(it + 1) * TT, :]
@@ -322,58 +382,131 @@ def tile_sinkhornattention_pa_t_kernel(tc, q_proj, k_proj, v, w_v, out):
             st["w_all"] = wide.tile([P, T], F32, name="w_all", tag="w8")
             nc.sync.dma_start(out=st["w_all"][:], in_=corner.rearrange("a p -> (a p)").partition_broadcast(P))
 
-        def round_steps(b, it):
-            st = state[b]
-            st["rho", it] = small.tile([P, NT], F32, name="rho")
-            if it == 0:
-                projection = value_projection(b)
-            else:
-                st["s_n", it] = small.tile([P, NT], F32, name="s_n")
-            steps = []
+        def first_round(b, projection):
+            state[b]["rho", 0] = rho_all[:, b, 0, :]
             for i in range(NT):
-                if it == 0:
-                    parts = [lambda i=i: exponent(b, i), lambda i=i: invert_first(b, i),
-                             lambda i=i: scale_first(b, i)]
-                    while len(parts) < 1:
-                        parts.append(None)
-                    parts[0] = lambda first=parts[0], i=i: [call() for call in (first, projection[i]) if call]
-                    sums, reduces, spreads, v_banks = 3, 3, 4, 4
-                else:
-                    parts = [lambda i=i: row_sum(b, it, i), lambda i=i: invert_scale(b, it, i)]
-                    sums, reduces, spreads, v_banks = 3, 3, 5, 2
-                    if it == ITERS - 1 and b % 2 == 1:
-                        sums, reduces, spreads = 3, 3, 3
-                extra = {}
-                extra.setdefault(sums, []).append(lambda i=i: column_sums(b, i, v_banks, it == 0))
-                if i == NT - 1:
-                    extra.setdefault(reduces, []).append(lambda: reduce_sums(b, v_banks))
-                    extra.setdefault(spreads, []).append(lambda: spread(b, it))
-                steps.append(merged(parts, [extra.get(d) and (lambda calls=extra[d]: [call() for call in calls])
-                                            for d in range(max(extra) + 1)]))
-            return steps
+                step(lambda i=i: (exponent(b, i), [call() for call in projection[i]]), lambda i=i: invert_first(b, i),
+                     lambda i=i: scale_first(b, i),
+                     lambda i=i: (column_sums(b, i, i == 0, i == NT - 1),
+                                  (scalar_sums(b, 4), reduce_sums(b, 4)) if i == NT - 1 else None),
+                     (lambda: spread(b, 0)) if i == NT - 1 else None)
 
-        def merged(parts, others):
-            both = []
-            for d in range(max(len(parts), len(others))):
-                calls = [side[d] for side in (parts, others) if d < len(side) and side[d]]
-                both.append((lambda calls=calls: [call() for call in calls]) if calls else None)
-            return both
+        def sums(b, *tiles):
+            for i in tiles:
+                column_sums(b, i, i == 0, i == 5)
+
+        def finish_rows(p, pit):
+            vector_scale(p, pit, 4)
+            vector_scale(p, pit, 5)
+
+        def flush():
+            if pending:
+                step()
+
+        def phase(b, it, p, pit, more):
+            row_sum(b, it, 0)
+            if not pit:
+                flush()
+            if pit:
+                invert_row(p, pit, 5)
+                vector_scale(p, pit, 4)
+            invert_row(b, it, 0)
+            if pit:
+                reduce_turned(b, it)
+            if not pit:
+                row_sum(b, it, 6)
+                flush()
+            if pit:
+                vector_scale(p, pit, 5)
+            if not pit:
+                row_sum(b, it, 7)
+            invert_turned(b, it)
+            if not pit:
+                flush()
+            scalar_scale(b, it, 0)
+            if pit:
+                sums(p, 3)
+                sums(p, 4)
+                sums(p, 5)
+            scalar_scale(b, it, 6)
+            row_sum(b, it, 1)
+            if not pit:
+                flush()
+            if pit:
+                reduce_sums(p, 4)
+                spread_invert(p)
+            invert_row(b, it, 1)
+            if pit:
+                spread(p, pit, True)
+            scalar_scale(b, it, 7)
+            if not pit:
+                flush()
+            if more:
+                turn_tiles(p, 0)
+                turn_tiles(p, 1)
+                turn_tiles(p, 2)
+            row_sum(b, it, 2)
+            sums(b, 0)
+            sums(b, 6)
+            if more:
+                weigh_tiles(p, 0)
+                weigh_tiles(p, 1)
+            scalar_scale(b, it, 1)
+            if more:
+                add_tiles(p, 0)
+                turn_tiles(p, 3)
+                add_tiles(p, 1)
+                turn_tiles(p, 4)
+            sums(b, 7)
+            row_sum(b, it, 3)
+            invert_row(b, it, 2)
+            if more:
+                weigh_tiles(p, 2)
+                weigh_tiles(p, 3)
+                weigh_tiles(p, 4)
+            sums(b, 1)
+            scalar_scale(b, it, 2)
+            if more:
+                add_tiles(p, 2)
+                turn_tiles(p, 5)
+                add_tiles(p, 3)
+                turn_tiles(p, 6)
+                add_tiles(p, 4)
+                turn_tiles(p, 7)
+            row_sum(b, it, 4)
+            invert_row(b, it, 3)
+            if more:
+                weigh_tiles(p, 5)
+                weigh_tiles(p, 6)
+                weigh_tiles(p, 7)
+            sums(b, 2)
+            scalar_scale(b, it, 3)
+            if more:
+                add_tiles(p, 5)
+                add_tiles(p, 6)
+                add_tiles(p, 7)
+            row_sum(b, it, 5)
+            invert_row(b, it, 4)
 
         def rounds(pair):
-            first_steps = round_steps(pair[0], 0)
-            second_steps = round_steps(pair[1], 0)
-            for parts in first_steps + second_steps[:NT - AHEAD]:
-                step(*parts)
-            ahead = round_steps(pair[0], 1)
-            for k in range(AHEAD):
-                step(*merged(second_steps[NT - AHEAD + k], ahead[k]))
-            for parts in ahead[AHEAD:]:
-                step(*parts)
-            for it in range(1, ITERS):
-                for b in pair:
-                    if (b, it) != (pair[0], 1):
-                        for parts in round_steps(b, it):
-                            step(*parts)
+            projections = value_projection(pair[0])
+            for b in pair:
+                first_round(b, projections[NT * (b % 2):])
+            for b in pair:
+                for it in range(ITERS):
+                    state[b]["rho", it] = rho_all[:, b, it % 2, :]
+                    state[b]["s_n", it] = s_all[:, b, it % 2, :]
+            for n in range(2 * (ITERS - 1)):
+                b, it = pair[n % 2], 1 + n // 2
+                p, pit = pair[1 - n % 2], (n + 1) // 2
+                phase(b, it, p, pit, pit + 1 < ITERS)
+            b, it = pair[1], ITERS - 1
+            invert_row(b, it, 5)
+            finish_rows(b, it)
+            sums(b, 3, 4, 5)
+            while len(pending) < 2:
+                pending.append([])
+            pending[1].append(lambda: (scalar_sums(b, 0), reduce_sums(b, 0), spread(b, it)))
 
         def plan(b, g, c):
             st = state[b]
@@ -404,7 +537,7 @@ def tile_sinkhornattention_pa_t_kernel(tc, q_proj, k_proj, v, w_v, out):
                         out=po[:, a, :],
                         lhsT=codes[:, c, a * P:(a + 1) * P].bitcast(FP8X4),
                         lhsT_scale=scales[:, c, a * P:(a + 1) * P],
-                        rhs=vp_codes[:, b, c, :].bitcast(FP8X4), rhs_scale=vp_scales[:, b, c, :],
+                        rhs=vp_codes[:, b % 2, c, :].bitcast(FP8X4), rhs_scale=vp_scales[:, b % 2, c, :],
                         start=(c == 0), stop=(c == 1))
             o_sb = wide.tile([P, 4, D], F32, name="o_sb")
             nc.scalar.copy(out=o_sb[:], in_=po[:])
@@ -478,7 +611,7 @@ def tile_sinkhornattention_pa_t_kernel(tc, q_proj, k_proj, v, w_v, out):
                     distances(b)
             if first == 0:
                 step(wv_step)
-            step(lambda b=first: v_load(b))
+            step(lambda b=first: (v_load(b, 0), v_load(b, 1)))
             rounds(pair)
         rest = attend(B - 2, ticks(B - 1, TAIL_BLOCKS), FIRST_TICK)
         for block in blocks(TAIL_BLOCKS):

@@ -204,7 +204,7 @@ def tile_sinkhornattention_pa_t_kernel(tc, q_proj, k_proj, v, w_v, out):
                 pk = ps.tile([P, 4, P], BF16, name="pk", tag="ps")
                 for a in range(4):
                     nc.tensor.transpose(pk[:, a, :], state[b]["k_sb"][:, 4 * g + a, :], ident_b[:])
-                if b == 0:
+                if b < 2:
                     nc.vector.tensor_copy(out=k_t[:, b, 4 * g:4 * g + 4, :], in_=pk[:])
                 else:
                     nc.scalar.copy(out=k_t[:, b, 4 * g:4 * g + 4, :], in_=pk[:])
@@ -259,10 +259,9 @@ def tile_sinkhornattention_pa_t_kernel(tc, q_proj, k_proj, v, w_v, out):
 
             def beside(i):
                 if i == 3 and b + 1 < B:
-                    square_keys(b + 1)
                     turn_keys(b + 1)
-                    if b + 2 < B:
-                        k_load(b + 2)
+                if i == 3 and b < 2:
+                    k_load(b + 2)
                 for tick in stream[2 * i:2 * i + 2]:
                     tick()
                 if i % 2 == 1 and i // 2 < len(mine):
@@ -297,13 +296,13 @@ def tile_sinkhornattention_pa_t_kernel(tc, q_proj, k_proj, v, w_v, out):
         def invert_row(b, it, i):
             nc.vector.reciprocal(out=state[b]["rho", it][:, i:i + 1], in_=state[b]["s_n", it][:, i:i + 1])
 
-        def scalar_scale(b, it, i):
-            nc.scalar.activation(out=rows(b, i), in_=rows(b, i), func=ACT.Copy,
+        def scalar_scale(b, it, i, begin=0):
+            nc.scalar.activation(out=rows(b, i)[:, begin:T], in_=rows(b, i)[:, begin:T], func=ACT.Copy,
                                  scale=state[b]["rho", it][:, i:i + 1])
 
-        def vector_scale(b, it, i):
-            nc.vector.tensor_scalar(out=rows(b, i), in0=rows(b, i), scalar1=state[b]["rho", it][:, i:i + 1],
-                                    scalar2=None, op0=ALU.mult)
+        def vector_scale(b, it, i, end=T):
+            nc.vector.tensor_scalar(out=rows(b, i)[:, 0:end], in0=rows(b, i)[:, 0:end],
+                                    scalar1=state[b]["rho", it][:, i:i + 1], scalar2=None, op0=ALU.mult)
 
         def turn_tiles(b, u):
             st = state[b]
@@ -409,7 +408,8 @@ def tile_sinkhornattention_pa_t_kernel(tc, q_proj, k_proj, v, w_v, out):
                 flush()
             if pit:
                 invert_row(p, pit, 5)
-                vector_scale(p, pit, 4)
+                vector_scale(p, pit, 4, 1280)
+                scalar_scale(p, pit, 4, 1280)
             invert_row(b, it, 0)
             if pit:
                 reduce_turned(b, it)
@@ -597,10 +597,12 @@ def tile_sinkhornattention_pa_t_kernel(tc, q_proj, k_proj, v, w_v, out):
             for s in range(8):
                 mine = stream[:2] if s >= first_tick else []
                 stream = stream[len(mine):]
-                step(lambda s=s, mine=mine: (plan_step(b, s // 2, s % 2), [tick() for tick in mine]))
+                step(lambda s=s, mine=mine: (plan_step(b, s // 2, s % 2), [tick() for tick in mine],
+                                             square_keys(b + 2 + s) if b == 0 and s < 2 else None))
             return stream
 
         turn_keys(0)
+        square_keys(1)
         for first in range(0, B, 2):
             pair = (first, first + 1)
             for b in pair:

@@ -512,10 +512,10 @@ def tile_sinkhornattention_pa_t_kernel(tc, q_proj, k_proj, v, w_v, out):
             st = state[b]
             grp = group.tile([P, 512, 4], BF16, name="grp", tag="g4", align_bytes=64)
             nc.vector.tensor_tensor(
-                out=grp[:].rearrange("p (r i) j -> p r j i", i=4),
-                in0=st["half"][c][:, :, g * 512:(g + 1) * 512].rearrange("p j (r i) -> p r j i", i=4),
-                in1=st["w_all"][:, g * 512:(g + 1) * 512].rearrange("p (r i) -> p r i", i=4)
-                .unsqueeze(2).to_broadcast([P, 128, 4, 4]),
+                out=grp[:].rearrange("p (r i) j -> p r j i", i=8),
+                in0=st["half"][c][:, :, g * 512:(g + 1) * 512].rearrange("p j (r i) -> p r j i", i=8),
+                in1=st["w_all"][:, g * 512:(g + 1) * 512].rearrange("p (r i) -> p r i", i=8)
+                .unsqueeze(2).to_broadcast([P, 64, 4, 8]),
                 op=ALU.mult)
             st["grp", g, c] = grp
 

@@ -103,10 +103,6 @@ def tile_sinkhornattention_pa_t_kernel(tc, q_proj, k_proj, v, w_v, out):
             nc.scalar.activation(out=drop[:], in_=q_sb[:, a, :], func=ACT.Square, accum_out=q2[:, a:a + 1])
             if a % 4 == 3:
                 nc.scalar.activation(out=nq2h[:, a - 3:a + 1], in_=q2[:, a - 3:a + 1], func=ACT.Copy, scale=-0.5)
-        k_sq = wide.tile([P, NT, D], F32, name="k_sq", tag="w8")
-        nc.vector.tensor_tensor(out=k_sq[:], in0=state[0]["k_sb"][:], in1=state[0]["k_sb"][:], op=ALU.mult)
-        nc.vector.tensor_reduce(out=k2[:, 0, :], in_=k_sq[:], axis=AX.X, op=ALU.add)
-        nc.vector.tensor_scalar(out=k2h[:, 0, :], in0=k2[:, 0, :], scalar1=0.5, scalar2=None, op0=ALU.mult)
 
         def wv_step():
             wv_sb = one.tile([P, 2, 2, D], BF16, name="wv_sb")
@@ -602,6 +598,10 @@ def tile_sinkhornattention_pa_t_kernel(tc, q_proj, k_proj, v, w_v, out):
             return stream
 
         turn_keys(0)
+        k_sq = wide.tile([P, NT, D], F32, name="k_sq", tag="w8")
+        nc.vector.tensor_tensor(out=k_sq[:], in0=state[0]["k_sb"][:], in1=state[0]["k_sb"][:], op=ALU.mult)
+        nc.vector.tensor_reduce(out=k2[:, 0, :], in_=k_sq[:], axis=AX.X, op=ALU.add)
+        nc.vector.tensor_scalar(out=k2h[:, 0, :], in0=k2[:, 0, :], scalar1=0.5, scalar2=None, op0=ALU.mult)
         square_keys(1)
         for first in range(0, B, 2):
             pair = (first, first + 1)

from contextlib import ExitStack

import concourse.mybir as mybir
from concourse.masks import make_identity

F32 = mybir.dt.float32
BF16 = mybir.dt.bfloat16
U32 = mybir.dt.uint32
U8 = mybir.dt.uint8
FP8X4 = mybir.dt.float8_e4m3fn_x4
ACT = mybir.ActivationFunctionType
ALU = mybir.AluOpType
AX = mybir.AxisListType

B, T, N, D, VD = 4, 2048, 1024, 128, 512
ITERS = 5
P = 128
NT = N // P
TT = T // P
V_BANKS = 3
ORDER = ((0, 1), (1, 1), (2, 1), (3, 1), (3, 0), (2, 0), (1, 0), (0, 0))
FIRST_TICK = 3
MID_BLOCKS, TAIL_BLOCKS = 3, 4
FLOPS = 2 * B * (2 * T * N * D + N * VD * D)


def tile_sinkhornattention_pa_t_kernel(tc, q_proj, k_proj, v, w_v, out):
    nc = tc.nc
    with ExitStack() as ctx:
        ctx.enter_context(tc.manual_schedule())
        const = ctx.enter_context(tc.tile_pool(name="const", bufs=1))
        kern = ctx.enter_context(tc.tile_pool(name="kern", bufs=4))
        group = ctx.enter_context(tc.tile_pool(name="group", bufs=4))
        mids = ctx.enter_context(tc.tile_pool(name="mids", bufs=4))
        small = ctx.enter_context(tc.tile_pool(name="small", bufs=4))
        wide = ctx.enter_context(tc.tile_pool(name="wide", bufs=2))
        one = ctx.enter_context(tc.tile_pool(name="one", bufs=1))
        keys = ctx.enter_context(tc.tile_pool(name="keys", bufs=2))
        vals = ctx.enter_context(tc.tile_pool(name="vals", bufs=2))
        coded = ctx.enter_context(tc.tile_pool(name="coded", bufs=3))
        scrap = ctx.enter_context(tc.tile_pool(name="scrap", bufs=3))
        ps_a = ctx.enter_context(tc.psum_pool(name="ps_a", bufs=4))
        ps = ctx.enter_context(tc.psum_pool(name="ps", bufs=4))

        ident_f = const.tile([P, P], F32, name="ident_f")
        make_identity(nc, ident_f[:])
        ident_b = const.tile([P, P], BF16, name="ident_b")
        make_identity(nc, ident_b[:])
        q_t = const.tile([P, T], BF16, name="q_t")
        nq2h = const.tile([P, TT], F32, name="nq2h")
        w_cols = const.tile([P, B, 32], F32, name="w_cols", align_bytes=64)
        rho_all = const.tile([P, B, 2, NT], F32, name="rho_all")
        s_all = const.tile([P, B, 2, NT], F32, name="s_all")
        nc.gpsimd.memset(w_cols[:], 1.0)
        k_t = const.tile([P, B, NT, P], BF16, name="k_t")
        k2 = const.tile([P, B, NT], F32, name="k2")
        k2h = const.tile([P, B, NT], F32, name="k2h")
        vp_codes = const.tile([P, 2, 2, P], U32, name="vp_codes", align_bytes=64)
        vp_scales = const.tile([P, 2, 2, P], U8, name="vp_scales", align_bytes=64)
        wv_codes = const.tile([P, D], U32, name="wv_codes", align_bytes=64)
        wv_scales = const.tile([P, D], U8, name="wv_scales", align_bytes=64)

        state = [dict() for b in range(B)]
        pending = []

        def step(*parts):
            for delay, part in enumerate(parts):
                while len(pending) <= delay:
                    pending.append([])
                if part is not None:
                    pending[delay].append(part)
            for part in reversed(pending.pop(0)):
                part()

        def later(part):
            if not pending:
                pending.append([])
            pending[0].append(part)

        def rows(b, i):
            return state[b]["half"][i // 4][:, i % 4, :]

        q_sb = group.tile([P, TT, D], BF16, name="q_sb", tag="g4", align_bytes=64)
        for g in range(0, TT, 8):
            nc.sync.dma_start(out=q_sb[:, g:g + 8, :], in_=q_proj.rearrange("(p a) d -> p a d", a=TT)[:, g:g + 8, :])

        def k_load(b):
            state[b]["k_sb"] = keys.tile([P, NT, D], BF16, name="k_sb")
            nc.sync.dma_start(
                out=state[b]["k_sb"][:].rearrange("p (c j) d -> p c j d", c=2),
                in_=k_proj[b].rearrange("(c p j) d -> p c j d", c=2, j=4))

        k_load(0)
        k_load(1)
        for g in range(4):
            pt = ps.tile([P, 512], BF16, name="pt", tag="ps")
            for a in range(4):
                nc.tensor.transpose(pt[:, a * P:(a + 1) * P], q_sb[:, 4 * g + a, :], ident_b[:])
            nc.vector.tensor_copy(out=q_t[:, g * 512:(g + 1) * 512], in_=pt[:])
        q2 = small.tile([P, TT], F32, name="q2")
        for a in range(TT):
            drop = small.tile([P, D], F32, name="drop")
            nc.scalar.activation(out=drop[:], in_=q_sb[:, a, :], func=ACT.Square, accum_out=q2[:, a:a + 1])
            if a % 4 == 3:
                nc.scalar.activation(out=nq2h[:, a - 3:a + 1], in_=q2[:, a - 3:a + 1], func=ACT.Copy, scale=-0.5)

        def wv_step():
            wv_sb = one.tile([P, 2, 2, D], BF16, name="wv_sb")
            nc.sync.dma_start(out=wv_sb[:], in_=w_v.rearrange("(u q e) c -> q u e c", u=2, e=2))
            wv_grp = one.tile([P, D, 4], BF16, name="wv_grp", align_bytes=64)
            nc.vector.tensor_copy(out=wv_grp[:], in_=wv_sb[:].rearrange("q u e c -> q c (u e)"))
            nc.vector.quantize_mx(
                out=wv_codes[:].bitcast(FP8X4), scales=wv_scales[:],
                in_=wv_grp[:].rearrange("q c t -> q (c t)"))

        def v_load(b, c):
            v_sb = vals.tile([P, 4, VD], BF16, name="v_sb")
            nc.sync.dma_start(
                out=v_sb[:], in_=v[b, c * 4 * P:(c + 1) * 4 * P, :].rearrange("(p j) f -> p j f", j=4))
            state[b]["v_sb", c] = v_sb

        def v_turn(b, c):
            st = state[b]
            for h in range(2):
                st["pv", h] = ps.tile([P, 2, 2, P], F32, name="pv", tag="ps")
                for jj in range(2):
                    words = st["v_sb", c][:, 2 * h + jj, :].bitcast(F32)
                    for u in range(2):
                        nc.tensor.transpose(st["pv", h][:, jj, u, :], words[:, u * P:(u + 1) * P], ident_f[:])

        def v_group(b):
            st = state[b]
            st["v_grp"] = group.tile([P, 4 * P * 4], BF16, name="v_grp", tag="g4", align_bytes=64)
            v_words = st["v_grp"][:].bitcast(F32).rearrange("q (j n u) -> q j n u", j=4, u=2)
            for h in range(2):
                nc.vector.tensor_copy(
                    out=v_words[:, 2 * h:2 * h + 2, :, :],
                    in_=st["pv", h][:].rearrange("q j u n -> q j n u"))

        def v_quantise(b):
            st = state[b]
            st["v_codes"] = coded.tile([P, 4 * P], U32, name="v_codes", tag="codes", align_bytes=64)
            st["v_scales"] = coded.tile([P, 4 * P], U8, name="v_scales", tag="scales", align_bytes=64)
            nc.vector.quantize_mx(out=st["v_codes"][:].bitcast(FP8X4), scales=st["v_scales"][:],
                                  in_=st["v_grp"][:])

        def v_multiply(b):
            st = state[b]
            st["pvp"] = ps.tile([P, 4, D], F32, name="pvp", tag="ps")
            for j in range(4):
                nc.tensor.matmul_mx(
                    out=st["pvp"][:, j, :],
                    lhsT=st["v_codes"][:, j * P:(j + 1) * P].bitcast(FP8X4),
                    lhsT_scale=st["v_scales"][:, j * P:(j + 1) * P],
                    rhs=wv_codes[:].bitcast(FP8X4), rhs_scale=wv_scales[:],
                    start=True, stop=True)

        def vp_group(b):
            st = state[b]
            st["vp_grp"] = one.tile([P, D, 4], BF16, name="vp_grp", align_bytes=64)
            nc.vector.tensor_copy(out=st["vp_grp"][:], in_=st["pvp"][:].rearrange("p j d -> p d j"))

        def vp_quantise(b, c):
            nc.vector.quantize_mx(
                out=vp_codes[:, b % 2, c, :].bitcast(FP8X4), scales=vp_scales[:, b % 2, c, :],
                in_=state[b]["vp_grp"][:].rearrange("p d j -> p (d j)"))

        def value_projection(first):
            halves = [(b, c) for b in (first, first + 1) for c in range(2)]

            def part(h, s):
                b, c = halves[h]
                if s == 0:
                    v_turn(b, c)
                elif s == 1:
                    v_group(b)
                    if h + 2 < len(halves):
                        v_load(*halves[h + 2])
                elif s == 2:
                    v_quantise(b)
                    v_multiply(b)
                else:
                    vp_group(b)
                    vp_quantise(b, c)
            beside = [[] for n in range(2 * NT)]
            for h in range(len(halves)):
                for s in range(4):
                    beside[2 * h + s + 0].insert(0, lambda h=h, s=s: part(h, s))
            return beside

        def square_keys(b):
            for i in range(NT):
                drop = small.tile([P, D], F32, name="drop")
                nc.scalar.activation(out=drop[:], in_=state[b]["k_sb"][:, i, :], func=ACT.Square,
                                     accum_out=k2[:, b, i:i + 1])
            nc.scalar.activation(out=k2h[:, b, :], in_=k2[:, b, :], func=ACT.Copy, scale=0.5)

        def turn_keys(b):
            for g in range(2):
                pk = ps.tile([P, 4, P], BF16, name="pk", tag="ps")
                for a in range(4):
                    nc.tensor.transpose(pk[:, a, :], state[b]["k_sb"][:, 4 * g + a, :], ident_b[:])
                if b < 2:
                    nc.vector.tensor_copy(out=k_t[:, b, 4 * g:4 * g + 4, :], in_=pk[:])
                else:
                    nc.scalar.copy(out=k_t[:, b, 4 * g:4 * g + 4, :], in_=pk[:])

        def dots(b, i):
            st = state[b]
            if i == 0:
                st["half"] = []
                st["y_max"] = small.tile([P, NT, 4], F32, name="y_max")
                st["s_first"] = small.tile([P, NT], F32, name="s_first")
            if i % 4 == 0:
                st["half"].append(kern.tile([P, 4, T], F32, name="half", tag="half"))
            wide_run = b != 2
            for pair_ch in ((0, 1, 2, 3),) if wide_run else ((0, 1), (2, 3)):
                banks = {}
                for ch in pair_ch:
                    if wide_run and i % 2 == 1:
                        pd = ps_a.tile([P, 512], F32, name="pd", tag="acc")
                    else:
                        pd = ps.tile([P, 512], F32, name="pd", tag="ps")
                    nc.tensor.matmul(pd[:], lhsT=k_t[:, b, i, :], rhs=q_t[:, ch * 512:(ch + 1) * 512],
                                     start=True, stop=False)
                    banks[ch] = pd
                for ch in pair_ch:
                    for a in range(4):
                        col = 4 * ch + a
                        nc.tensor.matmul(banks[ch][:, a * P:(a + 1) * P],
                                         lhsT=nq2h[:, col:col + 1].to_broadcast([P, P]), rhs=ident_f[:],
                                         is_transpose=True, start=False, stop=(a == 3))
                    nc.vector.tensor_scalar(out=rows(b, i)[:, ch * 512:(ch + 1) * 512], in0=banks[ch][:],
                                            scalar1=k2h[:, b, i:i + 1], scalar2=None,
                                            op0=ALU.min, op1=ALU.max, accum_out=st["y_max"][:, i, ch:ch + 1])

        def root(b, i):
            nc.scalar.activation(out=rows(b, i), in_=rows(b, i), func=ACT.Sqrt, bias=k2[:, b, i:i + 1],
                                 scale=-2.0)

        def shift_bound(b):
            st = state[b]
            y_top = small.tile([P, NT], F32, name="y_top")
            nc.vector.tensor_reduce(out=y_top[:], in_=st["y_max"][:], axis=AX.X, op=ALU.max)
            st["sq_min"] = small.tile([P, NT], F32, name="sq_min")
            nc.vector.scalar_tensor_tensor(out=st["sq_min"][:], in0=y_top[:], scalar=-2.0, in1=k2[:, b, :],
                                           op0=ALU.mult, op1=ALU.add)

        def shift_root(b):
            st = state[b]
            st["shift"] = small.tile([P, NT], F32, name="shift")
            nc.scalar.activation(out=st["shift"][:], in_=st["sq_min"][:], func=ACT.Sqrt)

        def distances(b, before=None, stream=(), mine=()):

            def beside(i):
                if i == 3 and b + 1 < B:
                    turn_keys(b + 1)
                if i == 3 and b < 2:
                    k_load(b + 2)
                for tick in stream[2 * i:2 * i + 2]:
                    tick()
                if i % 2 == 1 and i // 2 < len(mine):
                    plan_step(before, *mine[i // 2])

            for i in range(NT):
                step(lambda i=i: (dots(b, i), beside(i)),
                     lambda i=i: (root(b, i), shift_root(b) if i == NT - 1 else None))
            step(lambda: shift_bound(b))
            for block in mine[NT // 2:]:
                step(lambda block=block: plan_step(before, *block))

        def exponent(b, i):
            st = state[b]
            nc.scalar.activation(out=rows(b, i), in_=rows(b, i), func=ACT.Exp, bias=st["shift"][:, i:i + 1],
                                 scale=-1.0, accum_out=st["s_first"][:, i:i + 1])

        def row_sum(b, it, i):
            st = state[b]
            junk = scrap.tile([P, T], BF16, name="junk")
            nc.vector.scalar_tensor_tensor(
                out=junk[:], in0=rows(b, i), scalar=float(N), in1=st["w_all"][:],
                op0=ALU.mult, op1=ALU.mult, accum_out=st["s_n", it][:, i:i + 1])

        def invert_first(b, i):
            nc.vector.reciprocal(out=state[b]["rho", 0][:, i:i + 1], in_=state[b]["s_first"][:, i:i + 1])

        def scale_first(b, i):
            nc.vector.tensor_scalar(out=rows(b, i), in0=rows(b, i), scalar1=state[b]["rho", 0][:, i:i + 1],
                                    scalar2=1.0 / N, op0=ALU.mult, op1=ALU.mult)

        def invert_row(b, it, i):
            nc.vector.reciprocal(out=state[b]["rho", it][:, i:i + 1], in_=state[b]["s_n", it][:, i:i + 1])

        def scalar_scale(b, it, i, begin=0):
            nc.scalar.activation(out=rows(b, i)[:, begin:T], in_=rows(b, i)[:, begin:T], func=ACT.Copy,
                                 scale=state[b]["rho", it][:, i:i + 1])

        def vector_scale(b, it, i, end=T):
            nc.vector.tensor_scalar(out=rows(b, i)[:, 0:end], in0=rows(b, i)[:, 0:end],
                                    scalar1=state[b]["rho", it][:, i:i + 1], scalar2=None, op0=ALU.mult)

        def turn_tiles(b, u):
            st = state[b]
            st["turned", u % 4] = ps.tile([P, 2, 2, P], F32, name="turned", tag="ps")
            for h in range(2):
                for t in range(2):
                    a = 2 * u + h
                    nc.tensor.transpose(st["turned", u % 4][:, h, t, :], rows(b, NT - 2 + t)[:, a * P:(a + 1) * P],
                                        ident_f[:])

        def weigh_tiles(b, u):
            st = state[b]
            st["mid", u % 4] = mids.tile([P, 2, 2, P], F32, name="mid")
            for h in range(2):
                a = 2 * u + h
                nc.scalar.activation(out=st["mid", u % 4][:, h, :, :], in_=st["turned", u % 4][:, h, :, :],
                                     func=ACT.Copy, scale=w_cols[:, b, a:a + 1])

        def add_tiles(b, u):
            st = state[b]
            if u == 0:
                st["racc"] = ps.tile([P, 2, P], F32, name="racc", tag="ps")
            for h in range(2):
                for t in range(2):
                    nc.tensor.matmul(st["racc"][:, t, :], lhsT=st["mid", u % 4][:, h, t, :], rhs=ident_f[:],
                                     is_transpose=True, start=(u == 0 and h == 0 and t == 0),
                                     stop=(u == 7 and h == 1 and t == 1))

        def reduce_turned(b, it):
            for t in range(2):
                drop = small.tile([P, D], F32, name="drop")
                nc.vector.tensor_scalar(out=drop[:], in0=state[b]["racc"][:, t, :], scalar1=float(N), scalar2=None,
                                        op0=ALU.mult, op1=ALU.add,
                                        accum_out=state[b]["s_n", it][:, NT - 2 + t:NT - 1 + t])

        def invert_turned(b, it):
            nc.vector.reciprocal(out=state[b]["rho", it][:, NT - 2:NT], in_=state[b]["s_n", it][:, NT - 2:NT])


        def column_sums(b, i, first, last):
            st = state[b]
            if first:
                for g in range(4):
                    st["acc", g] = ps_a.tile([P, 4, P], F32, name="acc", tag="acc")
            for a in range(TT):
                nc.tensor.matmul(st["acc", a // 4][:, a % 4, :], lhsT=rows(b, i)[:, a * P:(a + 1) * P], rhs=ident_f[:],
                                 is_transpose=True,
                                 start=(first and a % 4 == 0), stop=(last and a % 4 == 3))

        def scalar_sums(b, v_banks):
            st = state[b]
            st["r_sum"] = small.tile([P, TT], F32, name="r_sum")
            for a in range(4 * v_banks, TT):
                drop = small.tile([P, D], F32, name="drop")
                nc.scalar.activation(out=drop[:], in_=st["acc", a // 4][:, a % 4, :], func=ACT.Copy,
                                     accum_out=st["r_sum"][:, a:a + 1])

        def reduce_sums(b, v_banks):
            st = state[b]
            for g in range(v_banks):
                nc.vector.tensor_reduce(out=st["r_sum"][:, 4 * g:4 * g + 4],
                                        in_=st["acc", g][:], axis=AX.X, op=ALU.add)

        def spread_invert(b):
            nc.vector.reciprocal(out=w_cols[:, b, 0:TT], in_=state[b]["r_sum"][:])

        def spread(b, it, inverted=False):
            st = state[b]
            if not inverted:
                spread_invert(b)
            w_turn = small.tile([P, 32], F32, name="w_turn", align_bytes=64)
            nc.vector.transpose(out=w_turn[:], in_=w_cols[:, b, :])
            corner = out[b, it * TT:(it + 1) * TT, :]
            for quad in range(0, P, 32):
                nc.sync.dma_start(out=corner[:, quad:quad + 32], in_=w_turn[quad:quad + TT, :])
            st["w_all"] = wide.tile([P, T], F32, name="w_all", tag="w8")
            nc.sync.dma_start(out=st["w_all"][:], in_=corner.rearrange("a p -> (a p)").partition_broadcast(P))

        def first_round(b, projection):
            state[b]["rho", 0] = rho_all[:, b, 0, :]
            for i in range(NT):
                step(lambda i=i: (exponent(b, i), [call() for call in projection[i]]), lambda i=i: invert_first(b, i),
                     lambda i=i: scale_first(b, i),
                     lambda i=i: (column_sums(b, i, i == 0, i == NT - 1),
                                  (scalar_sums(b, 4), reduce_sums(b, 4)) if i == NT - 1 else None),
                     (lambda: spread(b, 0)) if i == NT - 1 else None)

        def sums(b, *tiles):
            for i in tiles:
                column_sums(b, i, i == 0, i == 5)

        def finish_rows(p, pit):
            vector_scale(p, pit, 4)
            vector_scale(p, pit, 5)

        def flush():
            if pending:
                step()

        def phase(b, it, p, pit, more):
            row_sum(b, it, 0)
            if not pit:
                flush()
            if pit:
                invert_row(p, pit, 5)
                vector_scale(p, pit, 4, 1280)
                scalar_scale(p, pit, 4, 1280)
            invert_row(b, it, 0)
            if pit:
                reduce_turned(b, it)
            if not pit:
                row_sum(b, it, 6)
                flush()
            if pit:
                vector_scale(p, pit, 5)
            if not pit:
                row_sum(b, it, 7)
            invert_turned(b, it)
            if not pit:
                flush()
            scalar_scale(b, it, 0)
            if pit:
                sums(p, 3)
                sums(p, 4)
                sums(p, 5)
            scalar_scale(b, it, 6)
            row_sum(b, it, 1)
            if not pit:
                flush()
            if pit:
                reduce_sums(p, 4)
                spread_invert(p)
            invert_row(b, it, 1)
            if pit:
                spread(p, pit, True)
            scalar_scale(b, it, 7)
            if not pit:
                flush()
            if more:
                turn_tiles(p, 0)
                turn_tiles(p, 1)
                turn_tiles(p, 2)
            row_sum(b, it, 2)
            sums(b, 0)
            sums(b, 6)
            if more:
                weigh_tiles(p, 0)
                weigh_tiles(p, 1)
            scalar_scale(b, it, 1)
            if more:
                add_tiles(p, 0)
                turn_tiles(p, 3)
                add_tiles(p, 1)
                turn_tiles(p, 4)
            sums(b, 7)
            row_sum(b, it, 3)
            invert_row(b, it, 2)
            if more:
                weigh_tiles(p, 2)
                weigh_tiles(p, 3)
                weigh_tiles(p, 4)
            sums(b, 1)
            scalar_scale(b, it, 2)
            if more:
                add_tiles(p, 2)
                turn_tiles(p, 5)
                add_tiles(p, 3)
                turn_tiles(p, 6)
                add_tiles(p, 4)
                turn_tiles(p, 7)
            row_sum(b, it, 4)
            invert_row(b, it, 3)
            if more:
                weigh_tiles(p, 5)
                weigh_tiles(p, 6)
                weigh_tiles(p, 7)
            sums(b, 2)
            scalar_scale(b, it, 3)
            if more:
                add_tiles(p, 5)
                add_tiles(p, 6)
                add_tiles(p, 7)
            row_sum(b, it, 5)
            invert_row(b, it, 4)

        def rounds(pair):
            projections = value_projection(pair[0])
            for b in pair:
                first_round(b, projections[NT * (b % 2):])
            for b in pair:
                for it in range(ITERS):
                    state[b]["rho", it] = rho_all[:, b, it % 2, :]
                    state[b]["s_n", it] = s_all[:, b, it % 2, :]
            for n in range(2 * (ITERS - 1)):
                b, it = pair[n % 2], 1 + n // 2
                p, pit = pair[1 - n % 2], (n + 1) // 2
                phase(b, it, p, pit, pit + 1 < ITERS)
            b, it = pair[1], ITERS - 1
            invert_row(b, it, 5)
            finish_rows(b, it)
            sums(b, 3, 4, 5)
            while len(pending) < 2:
                pending.append([])
            pending[1].append(lambda: (scalar_sums(b, 0), reduce_sums(b, 0), spread(b, it)))

        def plan(b, g, c):
            st = state[b]
            grp = group.tile([P, 512, 4], BF16, name="grp", tag="g4", align_bytes=64)
            nc.vector.tensor_tensor(
                out=grp[:].rearrange("p (r i) j -> p r j i", i=8),
                in0=st["half"][c][:, :, g * 512:(g + 1) * 512].rearrange("p j (r i) -> p r j i", i=8),
                in1=st["w_all"][:, g * 512:(g + 1) * 512].rearrange("p (r i) -> p r i", i=8)
                .unsqueeze(2).to_broadcast([P, 64, 4, 8]),
                op=ALU.mult)
            st["grp", g, c] = grp

        def quantise(b, g, c):
            st = state[b]
            if ("codes", g) not in st:
                st["codes", g] = coded.tile([P, 2, 512], U32, name="codes", tag="codes", align_bytes=64)
                st["scales", g] = coded.tile([P, 2, 512], U8, name="scales", tag="scales", align_bytes=64)
            nc.vector.quantize_mx(out=st["codes", g][:, c, :].bitcast(FP8X4), scales=st["scales", g][:, c, :],
                                  in_=st["grp", g, c][:].rearrange("p t j -> p (t j)"))

        def multiply(b, g):
            codes = state[b]["codes", g]
            scales = state[b]["scales", g]
            po = ps.tile([P, 4, D], F32, name="po", tag="ps")
            for a in range(4):
                for c in range(2):
                    nc.tensor.matmul_mx(
                        out=po[:, a, :],
                        lhsT=codes[:, c, a * P:(a + 1) * P].bitcast(FP8X4),
                        lhsT_scale=scales[:, c, a * P:(a + 1) * P],
                        rhs=vp_codes[:, b % 2, c, :].bitcast(FP8X4), rhs_scale=vp_scales[:, b % 2, c, :],
                        start=(c == 0), stop=(c == 1))
            o_sb = wide.tile([P, 4, D], F32, name="o_sb")
            nc.scalar.copy(out=o_sb[:], in_=po[:])
            nc.sync.dma_start(out=out[b].rearrange("(p a) d -> p a d", a=TT)[:, 4 * g:4 * g + 4, :], in_=o_sb[:])

        def code(b, g, c):
            quantise(b, g, c)
            state[b]["coded", g] = state[b].get(("coded", g), 0) + 1
            if state[b]["coded", g] == 2:
                later(lambda: multiply(b, g))

        def plan_step(b, g, c):
            plan(b, g, c)
            later(lambda: code(b, g, c))

        def turn(b, g, c, a):
            st = state[b]
            if a == 0:
                st["grp", g, c] = group.tile([P, 512, 4], BF16, name="grp", tag="g4", align_bytes=64)
            st["turned"] = ps_a.tile([P, 4, P], F32, name="turned", tag="acc")
            cols = slice(g * 512 + a * P, g * 512 + (a + 1) * P)
            for j in range(4):
                nc.tensor.transpose(st["turned"][:, j, :], st["half"][c][:, j, cols], ident_f[:])

        def weigh(b, g, c, a):
            st = state[b]
            st["mid", a] = mids.tile([P, 4, P], F32, name="mid")
            nc.scalar.activation(out=st["mid", a][:], in_=st["turned"][:], func=ACT.Copy,
                                 scale=w_cols[:, b, 4 * g + a:4 * g + a + 1])

        def turn_back(b, g, c, a):
            st = state[b]
            back = ps_a.tile([P, 4, P], F32, name="back", tag="acc")
            for j in range(4):
                nc.tensor.transpose(back[:, j, :], st["mid", a][:, j, :], ident_f[:])
            nc.scalar.copy(out=st["grp", g, c][:, a * P:(a + 1) * P, :], in_=back[:].rearrange("p j t -> p t j"))
            if a == 3:
                later(lambda: code(b, g, c))

        def ticks(b, s_blocks):
            units = [(g, c, a) for g, c in ORDER[:s_blocks] for a in range(4)]

            def tick(u):
                if 0 <= u - 1 < len(units):
                    weigh(b, *units[u - 1])
                if u < len(units):
                    turn(b, *units[u])
                if 0 <= u - 2 < len(units):
                    turn_back(b, *units[u - 2])
            return [lambda u=u: tick(u) for u in range(len(units) + 2)]

        def blocks(s_blocks):
            return sorted(ORDER[s_blocks:])

        def attend(b, stream=(), first_tick=0):
            stream = list(stream)
            for s in range(8):
                mine = stream[:2] if s >= first_tick else []
                stream = stream[len(mine):]
                step(lambda s=s, mine=mine: (plan_step(b, s // 2, s % 2), [tick() for tick in mine],
                                             square_keys(b + 2 + s) if b == 0 and s < 2 else None))
            return stream

        turn_keys(0)
        k_sq = wide.tile([P, NT, D], F32, name="k_sq", tag="w8")
        nc.vector.tensor_tensor(out=k_sq[:], in0=state[0]["k_sb"][:], in1=state[0]["k_sb"][:], op=ALU.mult)
        nc.vector.tensor_reduce(out=k2[:, 0, :], in_=k_sq[:], axis=AX.X, op=ALU.add)
        nc.vector.tensor_scalar(out=k2h[:, 0, :], in0=k2[:, 0, :], scalar1=0.5, scalar2=None, op0=ALU.mult)
        square_keys(1)
        for first in range(0, B, 2):
            pair = (first, first + 1)
            for b in pair:
                if first > 0 and b == first:
                    rest = attend(b - 2, ticks(b - 1, MID_BLOCKS), FIRST_TICK)
                    distances(b, b - 1, rest, blocks(MID_BLOCKS))
                else:
                    distances(b)
            if first == 0:
                step(wv_step)
            step(lambda b=first: (v_load(b, 0), v_load(b, 1)))
            rounds(pair)
        rest = attend(B - 2, ticks(B - 1, TAIL_BLOCKS), FIRST_TICK)
        for block in blocks(TAIL_BLOCKS):
            step(lambda block=block, mine=rest[:2]: (plan_step(B - 1, *block), [tick() for tick in mine]))
            rest = rest[2:]
        for tick in rest:
            step(tick)
        while pending:
            step()
